import numpy as np
import ml_dtypes


def mxq(x, axis, fmt="e4m3"):
    dtype, down = {"e4m3": (ml_dtypes.float8_e4m3fn, 7), "e5m2": (ml_dtypes.float8_e5m2, 14)}[fmt]
    v = np.moveaxis(np.asarray(x, np.float32).astype(ml_dtypes.bfloat16).astype(np.float64), axis, -1)
    blocks = v.reshape(v.shape[:-1] + (-1, 32))
    amax = np.abs(blocks).max(-1, keepdims=True)
    byte = np.maximum(np.where(amax > 0, np.frexp(amax)[1] - 1 + 127, 0) - down, 1)
    scale = np.exp2(byte - 127.0)
    codes = (blocks / scale).astype(np.float32).astype(dtype).astype(np.float64)
    return np.moveaxis((codes * scale).reshape(v.shape), -1, axis)


WIDE = False


def mx_kscale(k):
    if not WIDE:
        return np.ones(k)
    levels = np.array([10, -10, 5, -5, 0])
    a = np.random.permutation(np.resize(levels, k // 512 * 4)).reshape(k // 512, 4)
    idx = np.arange(k)
    return np.exp2(a[idx // 512, idx % 128 // 32])


BF16 = ml_dtypes.bfloat16


def bf(x):
    return np.asarray(x, np.float32).astype(BF16)


def f64(x):
    return np.asarray(x).astype(np.float64)


E2M1 = np.array([0.0, 0.5, 1.0, 1.5, 2.0, 3.0, 4.0, 6.0, -0.0, -0.5, -1.0, -1.5, -2.0, -3.0, -4.0, -6.0])


def pack_weight(w, fmt):
    k, n = w.shape
    w = f64(bf(w)).reshape(k // 32, 32, n)
    amax = np.abs(w).max(1)
    if fmt == "e4m3":
        byte = np.frexp(amax)[1] - 1 + 127 - 7
    else:
        mant, ex = np.frexp(amax / 6.0)
        byte = np.where(mant > 0.5, ex, ex - 1) + 127
    byte = np.clip(np.where(amax > 0, byte, 1), 1, 254)
    scaled = (w * np.exp2(127.0 - byte)[:, None, :]).reshape(k, n).astype(np.float32)
    by_word = np.ascontiguousarray(scaled.reshape(k // 512, 128, 4, n).transpose(0, 1, 3, 2))
    if fmt == "e4m3":
        words = by_word.astype(ml_dtypes.float8_e4m3fn).view(np.uint8)
    else:
        c = by_word.astype(ml_dtypes.float4_e2m1fn).view(np.uint8) & 0xF
        words = c[..., 0::2] | (c[..., 1::2] << 4)
    return np.ascontiguousarray(words), np.ascontiguousarray(byte.astype(np.uint8).reshape(k // 512, 16, n))


def unpack_weight(words, scales, fmt):
    g, p, n, _ = words.shape
    if fmt == "e4m3":
        vals = np.ascontiguousarray(words).view(ml_dtypes.float8_e4m3fn).astype(np.float64)
    else:
        nib = np.empty((g, p, n, 4), np.uint8)
        nib[..., 0::2] = words & 0xF
        nib[..., 1::2] = words >> 4
        vals = E2M1[nib]
    vals = vals * np.repeat(np.exp2(scales.astype(np.float64) - 127.0), 8, axis=1)[..., None]
    return vals.transpose(0, 1, 3, 2).reshape(g * 512, n)


N, IN_DIM, HID, NUM_CLASSES, AVG_DEG = 1024, 512, 8192, 512, 32


def sigmoid(v):
    return 1.0 / (1.0 + np.exp(-v))


def setup_inputs():
    t = mx_kscale(HID)
    edges = np.random.uniform(size=(N, N)) < AVG_DEG / N
    A = bf(edges * (0.5 + np.random.uniform(size=(N, N))))
    deg_inv_sqrt = bf(1.0 / np.sqrt(1.0 + AVG_DEG * (0.75 + 0.5 * np.random.uniform(size=N))))
    h1 = bf(np.maximum(np.random.standard_normal((N, HID)) * 2.0 / np.sqrt(AVG_DEG), 0.0) * t)
    W2_words, W2_scales = pack_weight(np.random.standard_normal((HID, NUM_CLASSES)) * 4.0 / np.sqrt(HID) / t[:, None], "e4m3")
    b2 = bf(np.random.standard_normal(NUM_CLASSES) * 0.1)
    x = bf(np.random.standard_normal((N, NUM_CLASSES)) * 0.5)
    sigmoid_param = bf(4.0 + 0.4 * np.random.standard_normal(1))
    return {"A": A,
            "deg_inv_sqrt": deg_inv_sqrt,
            "h1": h1,
            "W2_words": W2_words,
            "W2_scales": W2_scales,
            "b2": b2,
            "x": x,
            "sigmoid_param": sigmoid_param}


def reference(A, deg_inv_sqrt, h1, W2_words, W2_scales, b2, x, sigmoid_param):
    dis = f64(deg_inv_sqrt)[:, None]
    g = mxq(f64(h1), 1, "e4m3") @ unpack_weight(W2_words, W2_scales, "e4m3")
    m = dis * g
    agg = mxq(f64(A), 0, "e4m3").T @ mxq(m, 0, "e4m3")
    h = dis * agg + dis ** 2 * g + f64(b2)
    return sigmoid(f64(sigmoid_param) * (h + f64(x)))

@@ -1,0 +1,304 @@
+from contextlib import ExitStack
+
+import concourse.mybir as mybir
+from concourse.masks import make_identity
+
+F32 = mybir.dt.float32
+BF16 = mybir.dt.bfloat16
+U8 = mybir.dt.uint8
+U32 = mybir.dt.uint32
+I32 = mybir.dt.int32
+FP8X4 = mybir.dt.float8_e4m3fn_x4
+ACT = mybir.ActivationFunctionType
+ALU = mybir.AluOpType
+
+P = 128
+PACK = 4
+K_PASS = P * PACK
+NODES, HIDDEN, CLASSES = 1024, 8192, 512
+HALVES = NODES // K_PASS
+TILES = HALVES * PACK
+GROUPS = HIDDEN // K_PASS
+CHUNK_GROUPS = 4
+CHUNKS = GROUPS // CHUNK_GROUPS
+CHUNK_K = CHUNK_GROUPS * K_PASS
+PAIR = 2
+PAIRS = PACK // PAIR
+ROUNDS = HALVES * CHUNKS * PAIRS
+UNITS = PAIR * CHUNK_GROUPS
+BANK_UNITS = 2
+GROUP_WORDS = K_PASS // 2
+H1_BUFS = 4
+
+FLOPS = 2 * NODES * HIDDEN * CLASSES + 2 * NODES * NODES * CLASSES
+
+
+def tile_gcnnodeclassifiernetwork_pb_k_kernel(
+    tc, A, deg_inv_sqrt, h1, W2_words, W2_scales, b2, x, sigmoid_param, out
+):
+    nc = tc.nc
+
+    h1_view = h1.rearrange("(h p t) k -> h p t k", p=P, t=PACK)
+    a_view = A.rearrange("(h p t) j -> h p t j", p=P, t=PACK)
+    x_view = x.rearrange("(h p t) n -> h p t n", p=P, t=PACK)
+    out_view = out.rearrange("(h p t) n -> h p t n", p=P, t=PACK)
+    d_view = deg_inv_sqrt.rearrange("(h p t) -> p h t", p=P, t=PACK)
+    w2_word_view = (
+        W2_words.rearrange("g p n t -> g p (n t)").bitcast(I32).rearrange("g p w -> p g w")
+    )
+    w2_scale_view = W2_scales.bitcast(I32).rearrange("g q w -> q g w")
+
+    with ExitStack() as ctx:
+        ctx.enter_context(tc.manual_schedule())
+        keep = ctx.enter_context(tc.tile_pool(name="keep", bufs=1))
+        h1_pool = ctx.enter_context(tc.tile_pool(name="h1_pool", bufs=H1_BUFS))
+        grouped_pool = ctx.enter_context(tc.tile_pool(name="grouped_pool", bufs=2))
+        codes_pool = ctx.enter_context(tc.tile_pool(name="codes_pool", bufs=3))
+        a_pool = ctx.enter_context(tc.tile_pool(name="a_pool", bufs=2))
+        out_pool = ctx.enter_context(tc.tile_pool(name="out_pool", bufs=3))
+        turn_banks = ctx.enter_context(tc.psum_pool(name="turn_banks", bufs=4))
+        sum_banks = ctx.enter_context(tc.psum_pool(name="sum_banks", bufs=4))
+
+        w2_codes = keep.tile([P, GROUPS, CLASSES], U32, name="w2_codes", align_bytes=64)
+        w2_planes = keep.tile([P, GROUPS, CLASSES], U8, name="w2_planes", align_bytes=64)
+        a_codes = keep.tile([P, HALVES, NODES], U32, name="a_codes", align_bytes=64)
+        a_planes = keep.tile([P, HALVES, NODES], U8, name="a_planes", align_bytes=64)
+        m_grouped = keep.tile([P, HALVES, CLASSES, PACK], BF16, name="m_grouped", align_bytes=64)
+        m_codes = keep.tile([P, HALVES, CLASSES], U32, name="m_codes", align_bytes=64)
+        m_planes = keep.tile([P, HALVES, CLASSES], U8, name="m_planes", align_bytes=64)
+        x_rows = keep.tile([P, TILES, CLASSES], BF16, name="x_rows")
+        rest = keep.tile([P, TILES, CLASSES], F32, name="rest")
+
+        nc.vector.memset(w2_planes[:].bitcast(I32), 0)
+        ident = keep.tile([P, P], F32, name="ident")
+        make_identity(nc, ident[:])
+        ones = keep.tile([P, P], BF16, name="ones")
+        nc.vector.memset(ones[:], 1.0)
+        b2_rows = keep.tile([P, CLASSES], BF16, name="b2_rows")
+        nc.vector.memset(b2_rows[:], 0.0)
+        nc.scalar.dma_start(out=b2_rows[0:1, :], in_=b2.unsqueeze(0))
+        d_bf = keep.tile([P, HALVES, PACK], BF16, name="d_bf")
+        nc.scalar.dma_start(out=d_bf[:], in_=d_view)
+        slope_bf = keep.tile([P, 1], BF16, name="slope_bf")
+        nc.scalar.dma_start(out=slope_bf[:], in_=sigmoid_param.partition_broadcast(P))
+        warm = keep.tile([P, 1], F32, name="warm")
+        nc.vector.memset(warm[:], 0.0)
+        nc.scalar.activation(out=warm[:], in_=warm[:], func=ACT.Sigmoid)
+
+        def load_h1(r):
+            half, chunk, pair = r // (CHUNKS * PAIRS), (r // PAIRS) % CHUNKS, r % PAIRS
+            raw = h1_pool.tile([P, PAIR, CHUNK_K], BF16, name="h1_raw")
+            nc.sync.dma_start(
+                out=raw[:],
+                in_=h1_view[
+                    half, :, PAIR * pair : PAIR * (pair + 1), CHUNK_K * chunk : CHUNK_K * (chunk + 1)
+                ],
+            )
+            return raw
+
+        def load_w2_scales():
+            for low_q in range(2):
+                for s in range(PACK):
+                    nc.sync.dma_start(
+                        out=w2_planes[32 * low_q + s : P : 64, :, :].bitcast(I32),
+                        in_=w2_scale_view[PACK * low_q + s : 16 : 8, :, :],
+                    )
+
+        def load_w2_chunk(chunk):
+            groups = slice(CHUNK_GROUPS * chunk, CHUNK_GROUPS * (chunk + 1))
+            nc.sync.dma_start(out=w2_codes[:, groups, :].bitcast(I32), in_=w2_word_view[:, groups, :])
+
+        a_raw = {}
+
+        def load_a(half):
+            a_raw[half] = a_pool.tile([P, PACK, NODES], BF16, name="a_raw")
+            nc.sync.dma_start(out=a_raw[half][:], in_=a_view[half])
+
+        def load_x(half):
+            nc.sync.dma_start(out=x_rows[:, PACK * half : PACK * (half + 1), :], in_=x_view[half])
+
+        h1_raw = {}
+
+        def load_round(r):
+            if r >= ROUNDS:
+                return
+            h1_raw[r] = load_h1(r)
+            if r % PAIRS != PAIRS - 1:
+                return
+            step = r // PAIRS
+            if step == 0:
+                load_w2_scales()
+            if step < CHUNKS:
+                load_w2_chunk(step)
+            if step == CHUNKS - 1:
+                load_x(0)
+            if CHUNKS <= step < CHUNKS + HALVES:
+                load_a(step - CHUNKS)
+            if step == CHUNKS + HALVES:
+                load_x(1)
+
+        grouped = {}
+
+        def transpose_round(r):
+            words = h1_raw[r][:].bitcast(F32)
+            grouped[r] = grouped_pool.tile([P, UNITS * K_PASS], BF16, name="grouped", align_bytes=64)
+            grouped_words = grouped[r][:].bitcast(F32).rearrange(
+                "p (n r u) -> p n r u", n=UNITS, u=2
+            )
+            for first in range(0, UNITS, BANK_UNITS):
+                bank = turn_banks.tile([P, BANK_UNITS, 2, P], F32, name="bank", tag="bank")
+                for i in range(BANK_UNITS):
+                    a, g = (first + i) // CHUNK_GROUPS, (first + i) % CHUNK_GROUPS
+                    for u in range(2):
+                        nc.tensor.transpose(
+                            bank[:, i, u, :],
+                            words[:, a, GROUP_WORDS * g + u : GROUP_WORDS * (g + 1) : 2],
+                            ident[:],
+                        )
+                nc.scalar.copy(
+                    out=grouped_words[:, first : first + BANK_UNITS, :, :],
+                    in_=bank[:].rearrange("p i u r -> p i r u"),
+                )
+
+        h1_codes = {}
+        h1_planes = {}
+
+        def quantise_round(r):
+            h1_codes[r] = codes_pool.tile([P, UNITS * P], U32, name="h1_codes", align_bytes=64)
+            h1_planes[r] = codes_pool.tile([P, UNITS * P], U8, name="h1_planes", align_bytes=64)
+            nc.vector.quantize_mx(
+                out=h1_codes[r][:].bitcast(FP8X4), scales=h1_planes[r][:], in_=grouped[r][:]
+            )
+
+        g_sum = {}
+
+        def multiply_round(r):
+            half, chunk, pair = r // (CHUNKS * PAIRS), (r // PAIRS) % CHUNKS, r % PAIRS
+            for a in range(PAIR):
+                tile_no = PACK * half + PAIR * pair + a
+                if chunk == 0:
+                    g_sum[tile_no] = sum_banks.tile([P, CLASSES], F32, name="g_sum", tag="sums")
+                for g in range(CHUNK_GROUPS):
+                    group = CHUNK_GROUPS * chunk + g
+                    cols = slice(P * (CHUNK_GROUPS * a + g), P * (CHUNK_GROUPS * a + g + 1))
+                    nc.tensor.matmul_mx(
+                        out=g_sum[tile_no][:],
+                        lhsT=h1_codes[r][:, cols].bitcast(FP8X4),
+                        lhsT_scale=h1_planes[r][:, cols],
+                        rhs=w2_codes[:, group, :].bitcast(FP8X4),
+                        rhs_scale=w2_planes[:, group, :],
+                        start=(group == 0),
+                        stop=(group == GROUPS - 1),
+                    )
+
+        def add_bias_to_skip(half):
+            for tile_no in range(PACK * half, PACK * (half + 1)):
+                nc.vector.tensor_tensor(
+                    out=rest[:, tile_no, :], in0=x_rows[:, tile_no, :], in1=b2_all[:], op=ALU.add
+                )
+
+        def leave_first_product(tile_no):
+            half, t = tile_no // PACK, tile_no % PACK
+            nc.scalar.activation(
+                out=m_grouped[:, half, :, t],
+                in_=g_sum[tile_no][:],
+                func=ACT.Copy,
+                scale=d[:, tile_no : tile_no + 1],
+            )
+            nc.vector.scalar_tensor_tensor(
+                out=rest[:, tile_no, :],
+                in0=g_sum[tile_no][:],
+                scalar=d_sq[:, tile_no : tile_no + 1],
+                in1=rest[:, tile_no, :],
+                op0=ALU.mult,
+                op1=ALU.add,
+            )
+
+        def quantise_m(half):
+            nc.vector.quantize_mx(
+                out=m_codes[:, half, :].bitcast(FP8X4),
+                scales=m_planes[:, half, :],
+                in_=m_grouped[:, half, :, :].rearrange("p n t -> p (n t)"),
+            )
+
+        def quantise_a(half, col_half):
+            cols = slice(K_PASS * col_half, K_PASS * (col_half + 1))
+            a_grouped = a_pool.tile([P, K_PASS * PACK], BF16, name="a_grouped", align_bytes=64)
+            nc.vector.tensor_copy(
+                out=a_grouped[:].rearrange("p (t2 p2 t) -> p t2 p2 t", t2=PACK, t=PACK),
+                in_=a_raw[half][:, :, cols].rearrange("p t (p2 t2) -> p t2 p2 t", t2=PACK),
+            )
+            nc.vector.quantize_mx(
+                out=a_codes[:, half, cols].bitcast(FP8X4),
+                scales=a_planes[:, half, cols],
+                in_=a_grouped[:],
+            )
+
+        agg = {}
+
+        def aggregate(tile_no, half):
+            cols = slice(P * tile_no, P * (tile_no + 1))
+            nc.tensor.matmul_mx(
+                out=agg[tile_no][:],
+                lhsT=a_codes[:, half, cols].bitcast(FP8X4),
+                lhsT_scale=a_planes[:, half, cols],
+                rhs=m_codes[:, half, :].bitcast(FP8X4),
+                rhs_scale=m_planes[:, half, :],
+                start=(half == 0),
+                stop=(half == HALVES - 1),
+            )
+
+        def finish(tile_no):
+            h_plus_x = out_pool.tile([P, CLASSES], F32, name="h_plus_x")
+            nc.vector.scalar_tensor_tensor(
+                out=h_plus_x[:],
+                in0=agg[tile_no][:],
+                scalar=d[:, tile_no : tile_no + 1],
+                in1=rest[:, tile_no, :],
+                op0=ALU.mult,
+                op1=ALU.add,
+            )
+            result = out_pool.tile([P, CLASSES], F32, name="result")
+            nc.scalar.activation(out=result[:], in_=h_plus_x[:], func=ACT.Sigmoid, scale=slope[:, 0:1])
+            nc.sync.dma_start(out=out_view[tile_no // PACK, :, tile_no % PACK, :], in_=result[:])
+
+        for r in range(H1_BUFS):
+            load_round(r)
+
+        b2_bank = turn_banks.tile([P, CLASSES], F32, name="b2_bank", tag="bank")
+        nc.tensor.matmul(out=b2_bank[:], lhsT=ones[:], rhs=b2_rows[:], start=True, stop=True)
+        b2_all = keep.tile([P, CLASSES], F32, name="b2_all")
+        nc.vector.tensor_copy(out=b2_all[:], in_=b2_bank[:])
+        d = keep.tile([P, TILES], F32, name="d")
+        nc.vector.tensor_copy(out=d[:], in_=d_bf[:].rearrange("p h t -> p (h t)"))
+        d_sq = keep.tile([P, TILES], F32, name="d_sq")
+        nc.vector.tensor_mul(out=d_sq[:], in0=d[:], in1=d[:])
+        slope = keep.tile([P, 1], F32, name="slope")
+        nc.vector.tensor_copy(out=slope[:], in_=slope_bf[:])
+
+        transpose_round(0)
+        load_round(H1_BUFS)
+        for r in range(ROUNDS):
+            half, chunk, pair = r // (CHUNKS * PAIRS), (r // PAIRS) % CHUNKS, r % PAIRS
+            if r + 1 < ROUNDS:
+                transpose_round(r + 1)
+                load_round(r + 1 + H1_BUFS)
+            quantise_round(r)
+            multiply_round(r)
+            if chunk == CHUNKS - 1:
+                if pair == 0:
+                    add_bias_to_skip(half)
+                for a in range(PAIR):
+                    leave_first_product(PACK * half + PAIR * pair + a)
+                if pair == PAIRS - 1:
+                    quantise_m(half)
+            if half == 1 and chunk < HALVES:
+                quantise_a(chunk, pair)
+
+        for tile_no in range(TILES):
+            banks, tag = (turn_banks, "bank") if tile_no < PACK else (sum_banks, "sums")
+            agg[tile_no] = banks.tile([P, CLASSES], F32, name="agg", tag=tag)
+            aggregate(tile_no, 0)
+        for tile_no in range(TILES):
+            aggregate(tile_no, 1)
+            finish(tile_no)

@@ -27,7 +27,6 @@ PAIRS = PACK // PAIR
 ROUNDS = HALVES * CHUNKS * PAIRS
 UNITS = PAIR * CHUNK_GROUPS
 BANK_UNITS = 2
-GROUP_WORDS = K_PASS // 2
 H1_BUFS = 4
 
 FLOPS = 2 * NODES * HIDDEN * CLASSES + 2 * NODES * NODES * CLASSES
@@ -52,6 +51,7 @@ def tile_gcnnodeclassifiernetwork_pb_k_kernel(
         ctx.enter_context(tc.manual_schedule())
         keep = ctx.enter_context(tc.tile_pool(name="keep", bufs=1))
         h1_pool = ctx.enter_context(tc.tile_pool(name="h1_pool", bufs=H1_BUFS))
+        sorted_pool = ctx.enter_context(tc.tile_pool(name="sorted_pool", bufs=2))
         grouped_pool = ctx.enter_context(tc.tile_pool(name="grouped_pool", bufs=2))
         codes_pool = ctx.enter_context(tc.tile_pool(name="codes_pool", bufs=3))
         a_pool = ctx.enter_context(tc.tile_pool(name="a_pool", bufs=2))
@@ -137,10 +137,20 @@ def tile_gcnnodeclassifiernetwork_pb_k_kernel(
             if step == CHUNKS + HALVES:
                 load_x(1)
 
+        sorted_words = {}
+
+        def sort_round(r):
+            sorted_words[r] = sorted_pool.tile([P, UNITS, 2, P], F32, name="sorted_words")
+            nc.vector.tensor_copy(
+                out=sorted_words[r][:],
+                in_=h1_raw[r][:].bitcast(F32).rearrange(
+                    "p a (g q u) -> p (a g) u q", g=CHUNK_GROUPS, u=2
+                ),
+            )
+
         grouped = {}
 
         def transpose_round(r):
-            words = h1_raw[r][:].bitcast(F32)
             grouped[r] = grouped_pool.tile([P, UNITS * K_PASS], BF16, name="grouped", align_bytes=64)
             grouped_words = grouped[r][:].bitcast(F32).rearrange(
                 "p (n r u) -> p n r u", n=UNITS, u=2
@@ -148,12 +158,9 @@ def tile_gcnnodeclassifiernetwork_pb_k_kernel(
             for first in range(0, UNITS, BANK_UNITS):
                 bank = turn_banks.tile([P, BANK_UNITS, 2, P], F32, name="bank", tag="bank")
                 for i in range(BANK_UNITS):
-                    a, g = (first + i) // CHUNK_GROUPS, (first + i) % CHUNK_GROUPS
                     for u in range(2):
                         nc.tensor.transpose(
-                            bank[:, i, u, :],
-                            words[:, a, GROUP_WORDS * g + u : GROUP_WORDS * (g + 1) : 2],
-                            ident[:],
+                            bank[:, i, u, :], sorted_words[r][:, first + i, u, :], ident[:]
                         )
                 nc.scalar.copy(
                     out=grouped_words[:, first : first + BANK_UNITS, :, :],
@@ -276,14 +283,18 @@ def tile_gcnnodeclassifiernetwork_pb_k_kernel(
         slope = keep.tile([P, 1], F32, name="slope")
         nc.vector.tensor_copy(out=slope[:], in_=slope_bf[:])
 
+        for r in range(2):
+            sort_round(r)
+            load_round(r + H1_BUFS)
         transpose_round(0)
-        load_round(H1_BUFS)
         for r in range(ROUNDS):
             half, chunk, pair = r // (CHUNKS * PAIRS), (r // PAIRS) % CHUNKS, r % PAIRS
             if r + 1 < ROUNDS:
                 transpose_round(r + 1)
-                load_round(r + 1 + H1_BUFS)
             quantise_round(r)
+            if r + 2 < ROUNDS:
+                sort_round(r + 2)
+                load_round(r + 2 + H1_BUFS)
             multiply_round(r)
             if chunk == CHUNKS - 1:
                 if pair == 0:

@@ -19,15 +19,16 @@ NODES, HIDDEN, CLASSES = 1024, 8192, 512
 HALVES = NODES // K_PASS
 TILES = HALVES * PACK
 GROUPS = HIDDEN // K_PASS
-CHUNK_GROUPS = 4
-CHUNKS = GROUPS // CHUNK_GROUPS
-CHUNK_K = CHUNK_GROUPS * K_PASS
-PAIR = 2
-PAIRS = PACK // PAIR
-ROUNDS = HALVES * CHUNKS * PAIRS
-UNITS = PAIR * CHUNK_GROUPS
-BANK_UNITS = 2
+ROUND_GROUPS = 8
+ROUND_K = ROUND_GROUPS * K_PASS
+PARTS = GROUPS // ROUND_GROUPS
+HALF_ROUNDS = PARTS * PACK
+ROUNDS = HALVES * HALF_ROUNDS
+BANK_GROUPS = 2
+PLANES = 4
 H1_BUFS = 4
+A_FIRST = HALF_ROUNDS
+X_FIRST = ROUNDS - TILES // 2
 
 FLOPS = 2 * NODES * HIDDEN * CLASSES + 2 * NODES * NODES * CLASSES
 
@@ -39,13 +40,13 @@ def tile_gcnnodeclassifiernetwork_pb_k_kernel(
 
     h1_view = h1.rearrange("(h p t) k -> h p t k", p=P, t=PACK)
     a_view = A.rearrange("(h p t) j -> h p t j", p=P, t=PACK)
-    x_view = x.rearrange("(h p t) n -> h p t n", p=P, t=PACK)
+    x_view = x.rearrange("(h p t) n -> p h (t n)", p=P, t=PACK)
     out_view = out.rearrange("(h p t) n -> h p t n", p=P, t=PACK)
     d_view = deg_inv_sqrt.rearrange("(h p t) -> p h t", p=P, t=PACK)
     w2_word_view = (
         W2_words.rearrange("g p n t -> g p (n t)").bitcast(I32).rearrange("g p w -> p g w")
     )
-    w2_scale_view = W2_scales.bitcast(I32).rearrange("g q w -> q g w")
+    w2_scale_view = W2_scales.bitcast(I32)
 
     with ExitStack() as ctx:
         ctx.enter_context(tc.manual_schedule())
@@ -60,7 +61,7 @@ def tile_gcnnodeclassifiernetwork_pb_k_kernel(
         sum_banks = ctx.enter_context(tc.psum_pool(name="sum_banks", bufs=4))
 
         w2_codes = keep.tile([P, GROUPS, CLASSES], U32, name="w2_codes", align_bytes=64)
-        w2_planes = keep.tile([P, GROUPS, CLASSES], U8, name="w2_planes", align_bytes=64)
+        w2_planes = keep.tile([P, GROUPS // PLANES, CLASSES], U8, name="w2_planes", align_bytes=64)
         a_codes = keep.tile([P, HALVES, NODES], U32, name="a_codes", align_bytes=64)
         a_planes = keep.tile([P, HALVES, NODES], U8, name="a_planes", align_bytes=64)
         m_grouped = keep.tile([P, HALVES, CLASSES, PACK], BF16, name="m_grouped", align_bytes=64)
@@ -85,94 +86,89 @@ def tile_gcnnodeclassifiernetwork_pb_k_kernel(
         nc.vector.memset(warm[:], 0.0)
         nc.scalar.activation(out=warm[:], in_=warm[:], func=ACT.Sigmoid)
 
-        def load_h1(r):
-            half, chunk, pair = r // (CHUNKS * PAIRS), (r // PAIRS) % CHUNKS, r % PAIRS
-            raw = h1_pool.tile([P, PAIR, CHUNK_K], BF16, name="h1_raw")
-            nc.sync.dma_start(
-                out=raw[:],
-                in_=h1_view[
-                    half, :, PAIR * pair : PAIR * (pair + 1), CHUNK_K * chunk : CHUNK_K * (chunk + 1)
-                ],
-            )
-            return raw
+        def where(r):
+            return r // HALF_ROUNDS, (r // PACK) % PARTS, r % PACK
 
-        def load_w2_scales():
-            for low_q in range(2):
-                for s in range(PACK):
-                    nc.sync.dma_start(
-                        out=w2_planes[32 * low_q + s : P : 64, :, :].bitcast(I32),
-                        in_=w2_scale_view[PACK * low_q + s : 16 : 8, :, :],
-                    )
+        def finished_in(r):
+            if r < 0 or r >= ROUNDS:
+                return None
+            half, part, t = where(r)
+            return PACK * half + t if part == PARTS - 1 else None
 
-        def load_w2_chunk(chunk):
-            groups = slice(CHUNK_GROUPS * chunk, CHUNK_GROUPS * (chunk + 1))
+        def load_w2(block):
+            groups = slice(PLANES * block, PLANES * (block + 1))
+            for quadrant in range(4):
+                nc.sync.dma_start(
+                    out=w2_planes[32 * quadrant : 32 * quadrant + 16, block, :].bitcast(I32),
+                    in_=w2_scale_view[groups, 4 * quadrant : 4 * quadrant + 4, :],
+                )
             nc.sync.dma_start(out=w2_codes[:, groups, :].bitcast(I32), in_=w2_word_view[:, groups, :])
 
         a_raw = {}
-
-        def load_a(half):
-            a_raw[half] = a_pool.tile([P, PACK, NODES], BF16, name="a_raw")
-            nc.sync.dma_start(out=a_raw[half][:], in_=a_view[half])
-
-        def load_x(half):
-            nc.sync.dma_start(out=x_rows[:, PACK * half : PACK * (half + 1), :], in_=x_view[half])
-
         h1_raw = {}
 
         def load_round(r):
             if r >= ROUNDS:
                 return
-            h1_raw[r] = load_h1(r)
-            if r % PAIRS != PAIRS - 1:
-                return
-            step = r // PAIRS
-            if step == 0:
-                load_w2_scales()
-            if step < CHUNKS:
-                load_w2_chunk(step)
-            if step == CHUNKS - 1:
-                load_x(0)
-            if CHUNKS <= step < CHUNKS + HALVES:
-                load_a(step - CHUNKS)
-            if step == CHUNKS + HALVES:
-                load_x(1)
+            half, part, t = where(r)
+            h1_raw[r] = h1_pool.tile([P, ROUND_K], BF16, name="h1_raw")
+            nc.sync.dma_start(
+                out=h1_raw[r][:], in_=h1_view[half, :, t, ROUND_K * part : ROUND_K * (part + 1)]
+            )
+            if half == 0 and t == 1:
+                for block in range(ROUND_GROUPS // PLANES):
+                    load_w2(ROUND_GROUPS // PLANES * part + block)
+            if half == 1 and r % 2 == 1:
+                late = (r - HALF_ROUNDS) // 2
+                if late < HALVES:
+                    a_raw[late] = a_pool.tile([P, PACK, NODES], BF16, name="a_raw")
+                    nc.sync.dma_start(out=a_raw[late][:], in_=a_view[late])
+                if late == HALVES:
+                    nc.sync.dma_start(
+                        out=x_rows[:].rearrange("p (h t) n -> p h (t n)", h=HALVES), in_=x_view
+                    )
 
         sorted_words = {}
 
         def sort_round(r):
-            sorted_words[r] = sorted_pool.tile([P, UNITS, 2, P], F32, name="sorted_words")
+            if r >= ROUNDS:
+                return
+            sorted_words[r] = sorted_pool.tile([P, ROUND_GROUPS, 2, P], F32, name="sorted_words")
             nc.vector.tensor_copy(
                 out=sorted_words[r][:],
-                in_=h1_raw[r][:].bitcast(F32).rearrange(
-                    "p a (g q u) -> p (a g) u q", g=CHUNK_GROUPS, u=2
-                ),
+                in_=h1_raw[r][:].bitcast(F32).rearrange("p (g q u) -> p g u q", g=ROUND_GROUPS, u=2),
             )
+            load_round(r + H1_BUFS)
 
         grouped = {}
 
         def transpose_round(r):
-            grouped[r] = grouped_pool.tile([P, UNITS * K_PASS], BF16, name="grouped", align_bytes=64)
+            if r >= ROUNDS:
+                return
+            grouped[r] = grouped_pool.tile([P, ROUND_K], BF16, name="grouped", align_bytes=64)
             grouped_words = grouped[r][:].bitcast(F32).rearrange(
-                "p (n r u) -> p n r u", n=UNITS, u=2
+                "p (g n u) -> p g n u", g=ROUND_GROUPS, u=2
             )
-            for first in range(0, UNITS, BANK_UNITS):
-                bank = turn_banks.tile([P, BANK_UNITS, 2, P], F32, name="bank", tag="bank")
-                for i in range(BANK_UNITS):
+            for first in range(0, ROUND_GROUPS, BANK_GROUPS):
+                bank = turn_banks.tile([P, BANK_GROUPS, 2, P], F32, name="bank", tag="bank")
+                for i in range(BANK_GROUPS):
                     for u in range(2):
                         nc.tensor.transpose(
                             bank[:, i, u, :], sorted_words[r][:, first + i, u, :], ident[:]
                         )
                 nc.scalar.copy(
-                    out=grouped_words[:, first : first + BANK_UNITS, :, :],
-                    in_=bank[:].rearrange("p i u r -> p i r u"),
+                    out=grouped_words[:, first : first + BANK_GROUPS, :, :],
+                    in_=bank[:].rearrange("p i u n -> p i n u"),
                 )
 
         h1_codes = {}
         h1_planes = {}
 
         def quantise_round(r):
-            h1_codes[r] = codes_pool.tile([P, UNITS * P], U32, name="h1_codes", align_bytes=64)
-            h1_planes[r] = codes_pool.tile([P, UNITS * P], U8, name="h1_planes", align_bytes=64)
+            if r >= ROUNDS:
+                return
+            h1_codes[r] = codes_pool.tile([P, ROUND_GROUPS * P], U32, name="h1_codes", align_bytes=64)
+            h1_planes[r] = codes_pool.tile([P, ROUND_GROUPS * P], U8, name="h1_planes", align_bytes=64)
             nc.vector.quantize_mx(
                 out=h1_codes[r][:].bitcast(FP8X4), scales=h1_planes[r][:], in_=grouped[r][:]
             )
@@ -180,38 +176,33 @@ def tile_gcnnodeclassifiernetwork_pb_k_kernel(
         g_sum = {}
 
         def multiply_round(r):
-            half, chunk, pair = r // (CHUNKS * PAIRS), (r // PAIRS) % CHUNKS, r % PAIRS
-            for a in range(PAIR):
-                tile_no = PACK * half + PAIR * pair + a
-                if chunk == 0:
-                    g_sum[tile_no] = sum_banks.tile([P, CLASSES], F32, name="g_sum", tag="sums")
-                for g in range(CHUNK_GROUPS):
-                    group = CHUNK_GROUPS * chunk + g
-                    cols = slice(P * (CHUNK_GROUPS * a + g), P * (CHUNK_GROUPS * a + g + 1))
-                    nc.tensor.matmul_mx(
-                        out=g_sum[tile_no][:],
-                        lhsT=h1_codes[r][:, cols].bitcast(FP8X4),
-                        lhsT_scale=h1_planes[r][:, cols],
-                        rhs=w2_codes[:, group, :].bitcast(FP8X4),
-                        rhs_scale=w2_planes[:, group, :],
-                        start=(group == 0),
-                        stop=(group == GROUPS - 1),
-                    )
-
-        def add_bias_to_skip(half):
-            for tile_no in range(PACK * half, PACK * (half + 1)):
-                nc.vector.tensor_tensor(
-                    out=rest[:, tile_no, :], in0=x_rows[:, tile_no, :], in1=b2_all[:], op=ALU.add
+            if r >= ROUNDS:
+                return
+            half, part, t = where(r)
+            tile_no = PACK * half + t
+            if part == 0:
+                g_sum[tile_no] = sum_banks.tile([P, CLASSES], F32, name="g_sum", tag="sums")
+            for g in range(ROUND_GROUPS):
+                group = ROUND_GROUPS * part + g
+                nc.tensor.matmul_mx(
+                    out=g_sum[tile_no][:],
+                    lhsT=h1_codes[r][:, P * g : P * (g + 1)].bitcast(FP8X4),
+                    lhsT_scale=h1_planes[r][:, P * g : P * (g + 1)],
+                    rhs=w2_codes[:, group, :].bitcast(FP8X4),
+                    rhs_scale=w2_planes[4 * (group % PLANES) : P, group // PLANES, :],
+                    start=(group == 0),
+                    stop=(group == GROUPS - 1),
                 )
 
-        def leave_first_product(tile_no):
-            half, t = tile_no // PACK, tile_no % PACK
+        def make_message(tile_no):
             nc.scalar.activation(
-                out=m_grouped[:, half, :, t],
+                out=m_grouped[:, tile_no // PACK, :, tile_no % PACK],
                 in_=g_sum[tile_no][:],
                 func=ACT.Copy,
                 scale=d[:, tile_no : tile_no + 1],
             )
+
+        def add_self_loop(tile_no):
             nc.vector.scalar_tensor_tensor(
                 out=rest[:, tile_no, :],
                 in0=g_sum[tile_no][:],
@@ -221,6 +212,11 @@ def tile_gcnnodeclassifiernetwork_pb_k_kernel(
                 op1=ALU.add,
             )
 
+        def add_skip(tile_no):
+            nc.vector.tensor_tensor(
+                out=rest[:, tile_no, :], in0=rest[:, tile_no, :], in1=x_rows[:, tile_no, :], op=ALU.add
+            )
+
         def quantise_m(half):
             nc.vector.quantize_mx(
                 out=m_codes[:, half, :].bitcast(FP8X4),
@@ -228,22 +224,33 @@ def tile_gcnnodeclassifiernetwork_pb_k_kernel(
                 in_=m_grouped[:, half, :, :].rearrange("p n t -> p (n t)"),
             )
 
-        def quantise_a(half, col_half):
-            cols = slice(K_PASS * col_half, K_PASS * (col_half + 1))
-            a_grouped = a_pool.tile([P, K_PASS * PACK], BF16, name="a_grouped", align_bytes=64)
-            nc.vector.tensor_copy(
-                out=a_grouped[:].rearrange("p (t2 p2 t) -> p t2 p2 t", t2=PACK, t=PACK),
-                in_=a_raw[half][:, :, cols].rearrange("p t (p2 t2) -> p t2 p2 t", t2=PACK),
+        a_grouped = {}
+
+        def regroup_a(quarter):
+            half, c = quarter // HALVES, quarter % HALVES
+            a_grouped[quarter] = a_pool.tile([P, K_PASS * PACK], BF16, name="a_grouped", align_bytes=64)
+            dst = a_grouped[quarter][:].rearrange("p (t2 p2 t) -> p t2 p2 t", t2=PACK, t=PACK)
+            src = a_raw[half][:, :, K_PASS * c : K_PASS * (c + 1)].rearrange(
+                "p t (p2 t2) -> p t2 p2 t", t2=PACK
             )
+            nc.scalar.copy(out=dst[:, 0:2, :, :], in_=src[:, 0:2, :, :])
+            nc.vector.tensor_copy(out=dst[:, 2:4, :, :], in_=src[:, 2:4, :, :])
+
+        def quantise_a(quarter):
+            half, c = quarter // HALVES, quarter % HALVES
+            cols = slice(K_PASS * c, K_PASS * (c + 1))
             nc.vector.quantize_mx(
                 out=a_codes[:, half, cols].bitcast(FP8X4),
                 scales=a_planes[:, half, cols],
-                in_=a_grouped[:],
+                in_=a_grouped[quarter][:],
             )
 
         agg = {}
 
         def aggregate(tile_no, half):
+            if half == 0:
+                banks, tag = (turn_banks, "bank") if tile_no < PACK else (sum_banks, "sums")
+                agg[tile_no] = banks.tile([P, CLASSES], F32, name="agg", tag=tag)
             cols = slice(P * tile_no, P * (tile_no + 1))
             nc.tensor.matmul_mx(
                 out=agg[tile_no][:],
@@ -283,33 +290,37 @@ def tile_gcnnodeclassifiernetwork_pb_k_kernel(
         slope = keep.tile([P, 1], F32, name="slope")
         nc.vector.tensor_copy(out=slope[:], in_=slope_bf[:])
 
-        for r in range(2):
-            sort_round(r)
-            load_round(r + H1_BUFS)
+        sort_round(0)
+        sort_round(1)
         transpose_round(0)
-        for r in range(ROUNDS):
-            half, chunk, pair = r // (CHUNKS * PAIRS), (r // PAIRS) % CHUNKS, r % PAIRS
-            if r + 1 < ROUNDS:
-                transpose_round(r + 1)
+        for r in range(ROUNDS + 2):
+            transpose_round(r + 1)
             quantise_round(r)
-            if r + 2 < ROUNDS:
-                sort_round(r + 2)
-                load_round(r + 2 + H1_BUFS)
+            sort_round(r + 2)
             multiply_round(r)
-            if chunk == CHUNKS - 1:
-                if pair == 0:
-                    add_bias_to_skip(half)
-                for a in range(PAIR):
-                    leave_first_product(PACK * half + PAIR * pair + a)
-                if pair == PAIRS - 1:
-                    quantise_m(half)
-            if half == 1 and chunk < HALVES:
-                quantise_a(chunk, pair)
+            if finished_in(r - 1) is not None:
+                make_message(finished_in(r - 1))
+            if finished_in(r - 2) is not None:
+                if finished_in(r - 2) % PACK == PACK - 1:
+                    quantise_m(finished_in(r - 2) // PACK)
+                add_self_loop(finished_in(r - 2))
+            if r == 1:
+                nc.vector.tensor_copy(
+                    out=rest[:], in_=b2_all[:].unsqueeze(1).to_broadcast([P, TILES, CLASSES])
+                )
+            if 0 <= r - A_FIRST - 1 < HALVES * HALVES:
+                quantise_a(r - A_FIRST - 1)
+            if 0 <= r - A_FIRST < HALVES * HALVES:
+                regroup_a(r - A_FIRST)
+            if X_FIRST <= r < ROUNDS:
+                add_skip(2 * (r - X_FIRST))
+                add_skip(2 * (r - X_FIRST) + 1)
 
-        for tile_no in range(TILES):
-            banks, tag = (turn_banks, "bank") if tile_no < PACK else (sum_banks, "sums")
-            agg[tile_no] = banks.tile([P, CLASSES], F32, name="agg", tag=tag)
+        for tile_no in range(TILES - 1):
             aggregate(tile_no, 0)
-        for tile_no in range(TILES):
+        for tile_no in range(TILES - 1):
             aggregate(tile_no, 1)
             finish(tile_no)
+        aggregate(TILES - 1, 0)
+        aggregate(TILES - 1, 1)
+        finish(TILES - 1)

@@ -27,7 +27,7 @@ ROUNDS = HALVES * HALF_ROUNDS
 BANK_GROUPS = 2
 PLANES = 4
 H1_BUFS = 4
-A_FIRST = HALF_ROUNDS
+A_FIRST = HALF_ROUNDS + 1
 X_FIRST = ROUNDS - TILES // 2
 
 FLOPS = 2 * NODES * HIDDEN * CLASSES + 2 * NODES * NODES * CLASSES
@@ -46,7 +46,7 @@ def tile_gcnnodeclassifiernetwork_pb_k_kernel(
     w2_word_view = (
         W2_words.rearrange("g p n t -> g p (n t)").bitcast(I32).rearrange("g p w -> p g w")
     )
-    w2_scale_view = W2_scales.bitcast(I32)
+    w2_scale_view = W2_scales.bitcast(F32)
 
     with ExitStack() as ctx:
         ctx.enter_context(tc.manual_schedule())
@@ -95,13 +95,17 @@ def tile_gcnnodeclassifiernetwork_pb_k_kernel(
             half, part, t = where(r)
             return PACK * half + t if part == PARTS - 1 else None
 
+        for block in range(GROUPS // PLANES):
+            for quadrant in range(4):
+                nc.gpsimd.dma_start(
+                    out=w2_planes[32 * quadrant : 32 * quadrant + 16, block, :].bitcast(F32),
+                    in_=w2_scale_view[
+                        PLANES * block : PLANES * (block + 1), 4 * quadrant : 4 * quadrant + 4, :
+                    ],
+                )
+
         def load_w2(block):
             groups = slice(PLANES * block, PLANES * (block + 1))
-            for quadrant in range(4):
-                nc.sync.dma_start(
-                    out=w2_planes[32 * quadrant : 32 * quadrant + 16, block, :].bitcast(I32),
-                    in_=w2_scale_view[groups, 4 * quadrant : 4 * quadrant + 4, :],
-                )
             nc.sync.dma_start(out=w2_codes[:, groups, :].bitcast(I32), in_=w2_word_view[:, groups, :])
 
         a_raw = {}

@@ -25,9 +25,15 @@ PARTS = GROUPS // ROUND_GROUPS
 HALF_ROUNDS = PARTS * PACK
 ROUNDS = HALVES * HALF_ROUNDS
 BANK_GROUPS = 2
+QUADRANT = 32
+QUADRANTS = P // QUADRANT
 PLANES = 4
+W2_BLOCKS = GROUPS // PLANES
+A_QUARTERS = HALVES * HALVES
+AHEAD = 2
 H1_BUFS = 4
-A_FIRST = HALF_ROUNDS + 1
+B2_STEP = 1
+A_FIRST = HALF_ROUNDS
 X_FIRST = ROUNDS - TILES // 2
 
 FLOPS = 2 * NODES * HIDDEN * CLASSES + 2 * NODES * NODES * CLASSES
@@ -46,7 +52,7 @@ def tile_gcnnodeclassifiernetwork_pb_k_kernel(
     w2_word_view = (
         W2_words.rearrange("g p n t -> g p (n t)").bitcast(I32).rearrange("g p w -> p g w")
     )
-    w2_scale_view = W2_scales.bitcast(F32)
+    w2_scale_view = W2_scales.bitcast(I32)
 
     with ExitStack() as ctx:
         ctx.enter_context(tc.manual_schedule())
@@ -54,14 +60,14 @@ def tile_gcnnodeclassifiernetwork_pb_k_kernel(
         h1_pool = ctx.enter_context(tc.tile_pool(name="h1_pool", bufs=H1_BUFS))
         sorted_pool = ctx.enter_context(tc.tile_pool(name="sorted_pool", bufs=2))
         grouped_pool = ctx.enter_context(tc.tile_pool(name="grouped_pool", bufs=2))
-        codes_pool = ctx.enter_context(tc.tile_pool(name="codes_pool", bufs=3))
+        codes_pool = ctx.enter_context(tc.tile_pool(name="codes_pool", bufs=AHEAD + 2))
         a_pool = ctx.enter_context(tc.tile_pool(name="a_pool", bufs=2))
         out_pool = ctx.enter_context(tc.tile_pool(name="out_pool", bufs=3))
         turn_banks = ctx.enter_context(tc.psum_pool(name="turn_banks", bufs=4))
         sum_banks = ctx.enter_context(tc.psum_pool(name="sum_banks", bufs=4))
 
         w2_codes = keep.tile([P, GROUPS, CLASSES], U32, name="w2_codes", align_bytes=64)
-        w2_planes = keep.tile([P, GROUPS // PLANES, CLASSES], U8, name="w2_planes", align_bytes=64)
+        w2_planes = keep.tile([P, W2_BLOCKS, CLASSES], U8, name="w2_planes", align_bytes=64)
         a_codes = keep.tile([P, HALVES, NODES], U32, name="a_codes", align_bytes=64)
         a_planes = keep.tile([P, HALVES, NODES], U8, name="a_planes", align_bytes=64)
         m_grouped = keep.tile([P, HALVES, CLASSES, PACK], BF16, name="m_grouped", align_bytes=64)
@@ -95,17 +101,14 @@ def tile_gcnnodeclassifiernetwork_pb_k_kernel(
             half, part, t = where(r)
             return PACK * half + t if part == PARTS - 1 else None
 
-        for block in range(GROUPS // PLANES):
-            for quadrant in range(4):
-                nc.gpsimd.dma_start(
-                    out=w2_planes[32 * quadrant : 32 * quadrant + 16, block, :].bitcast(F32),
-                    in_=w2_scale_view[
-                        PLANES * block : PLANES * (block + 1), 4 * quadrant : 4 * quadrant + 4, :
-                    ],
-                )
-
         def load_w2(block):
             groups = slice(PLANES * block, PLANES * (block + 1))
+            for quadrant in range(QUADRANTS):
+                rows = slice(QUADRANT * quadrant, QUADRANT * quadrant + PLANES * PACK)
+                nc.sync.dma_start(
+                    out=w2_planes[rows, block, :].bitcast(I32),
+                    in_=w2_scale_view[groups, PACK * quadrant : PACK * (quadrant + 1), :],
+                )
             nc.sync.dma_start(out=w2_codes[:, groups, :].bitcast(I32), in_=w2_word_view[:, groups, :])
 
         a_raw = {}
@@ -119,7 +122,7 @@ def tile_gcnnodeclassifiernetwork_pb_k_kernel(
             nc.sync.dma_start(
                 out=h1_raw[r][:], in_=h1_view[half, :, t, ROUND_K * part : ROUND_K * (part + 1)]
             )
-            if half == 0 and t == 1:
+            if half == 0 and t == AHEAD:
                 for block in range(ROUND_GROUPS // PLANES):
                     load_w2(ROUND_GROUPS // PLANES * part + block)
             if half == 1 and r % 2 == 1:
@@ -193,7 +196,7 @@ def tile_gcnnodeclassifiernetwork_pb_k_kernel(
                     lhsT=h1_codes[r][:, P * g : P * (g + 1)].bitcast(FP8X4),
                     lhsT_scale=h1_planes[r][:, P * g : P * (g + 1)],
                     rhs=w2_codes[:, group, :].bitcast(FP8X4),
-                    rhs_scale=w2_planes[4 * (group % PLANES) : P, group // PLANES, :],
+                    rhs_scale=w2_planes[PACK * (group % PLANES) : P, group // PLANES, :],
                     start=(group == 0),
                     stop=(group == GROUPS - 1),
                 )
@@ -237,8 +240,8 @@ def tile_gcnnodeclassifiernetwork_pb_k_kernel(
             src = a_raw[half][:, :, K_PASS * c : K_PASS * (c + 1)].rearrange(
                 "p t (p2 t2) -> p t2 p2 t", t2=PACK
             )
-            nc.scalar.copy(out=dst[:, 0:2, :, :], in_=src[:, 0:2, :, :])
-            nc.vector.tensor_copy(out=dst[:, 2:4, :, :], in_=src[:, 2:4, :, :])
+            nc.scalar.copy(out=dst[:, 0 : PACK // 2, :, :], in_=src[:, 0 : PACK // 2, :, :])
+            nc.vector.tensor_copy(out=dst[:, PACK // 2 : PACK, :, :], in_=src[:, PACK // 2 : PACK, :, :])
 
         def quantise_a(quarter):
             half, c = quarter // HALVES, quarter % HALVES
@@ -294,13 +297,16 @@ def tile_gcnnodeclassifiernetwork_pb_k_kernel(
         slope = keep.tile([P, 1], F32, name="slope")
         nc.vector.tensor_copy(out=slope[:], in_=slope_bf[:])
 
-        sort_round(0)
-        sort_round(1)
-        transpose_round(0)
-        for r in range(ROUNDS + 2):
-            transpose_round(r + 1)
+        for r in range(AHEAD + 1):
+            sort_round(r)
+        for r in range(AHEAD):
+            transpose_round(r)
+        for r in range(AHEAD - 1):
             quantise_round(r)
-            sort_round(r + 2)
+        for r in range(ROUNDS + 2):
+            transpose_round(r + AHEAD)
+            quantise_round(r + AHEAD - 1)
+            sort_round(r + AHEAD + 1)
             multiply_round(r)
             if finished_in(r - 1) is not None:
                 make_message(finished_in(r - 1))
@@ -308,13 +314,13 @@ def tile_gcnnodeclassifiernetwork_pb_k_kernel(
                 if finished_in(r - 2) % PACK == PACK - 1:
                     quantise_m(finished_in(r - 2) // PACK)
                 add_self_loop(finished_in(r - 2))
-            if r == 1:
+            if r == B2_STEP:
                 nc.vector.tensor_copy(
                     out=rest[:], in_=b2_all[:].unsqueeze(1).to_broadcast([P, TILES, CLASSES])
                 )
-            if 0 <= r - A_FIRST - 1 < HALVES * HALVES:
+            if 0 <= r - A_FIRST - 1 < A_QUARTERS:
                 quantise_a(r - A_FIRST - 1)
-            if 0 <= r - A_FIRST < HALVES * HALVES:
+            if 0 <= r - A_FIRST < A_QUARTERS:
                 regroup_a(r - A_FIRST)
             if X_FIRST <= r < ROUNDS:
                 add_skip(2 * (r - X_FIRST))

@@ -30,11 +30,16 @@ QUADRANTS = P // QUADRANT
 PLANES = 4
 W2_BLOCKS = GROUPS // PLANES
 A_QUARTERS = HALVES * HALVES
+W2_AFTER = 2
+SMALL_AFTER = 3
+CONST_STEP = 4
+LEAD_STEPS = 4
+WARM_UP = 8
 AHEAD = 2
 H1_BUFS = 4
-B2_STEP = 1
 A_FIRST = HALF_ROUNDS
 X_FIRST = ROUNDS - TILES // 2
+X_ORDER = (2, 3, 0, 1)
 
 FLOPS = 2 * NODES * HIDDEN * CLASSES + 2 * NODES * NODES * CLASSES
 
@@ -81,13 +86,16 @@ def tile_gcnnodeclassifiernetwork_pb_k_kernel(
         make_identity(nc, ident[:])
         ones = keep.tile([P, P], BF16, name="ones")
         nc.vector.memset(ones[:], 1.0)
+        warm_rows = keep.tile([P, CLASSES], BF16, name="warm_rows")
+        nc.vector.memset(warm_rows[:], 1.0)
         b2_rows = keep.tile([P, CLASSES], BF16, name="b2_rows")
         nc.vector.memset(b2_rows[:], 0.0)
-        nc.scalar.dma_start(out=b2_rows[0:1, :], in_=b2.unsqueeze(0))
         d_bf = keep.tile([P, HALVES, PACK], BF16, name="d_bf")
-        nc.scalar.dma_start(out=d_bf[:], in_=d_view)
         slope_bf = keep.tile([P, 1], BF16, name="slope_bf")
-        nc.scalar.dma_start(out=slope_bf[:], in_=sigmoid_param.partition_broadcast(P))
+        b2_all = keep.tile([P, CLASSES], F32, name="b2_all")
+        d = keep.tile([P, TILES], F32, name="d")
+        d_sq = keep.tile([P, TILES], F32, name="d_sq")
+        slope = keep.tile([P, 1], F32, name="slope")
         warm = keep.tile([P, 1], F32, name="warm")
         nc.vector.memset(warm[:], 0.0)
         nc.scalar.activation(out=warm[:], in_=warm[:], func=ACT.Sigmoid)
@@ -122,7 +130,11 @@ def tile_gcnnodeclassifiernetwork_pb_k_kernel(
             nc.sync.dma_start(
                 out=h1_raw[r][:], in_=h1_view[half, :, t, ROUND_K * part : ROUND_K * (part + 1)]
             )
-            if half == 0 and t == AHEAD:
+            if r == SMALL_AFTER:
+                nc.sync.dma_start(out=d_bf[:], in_=d_view)
+                nc.sync.dma_start(out=b2_rows[0:1, :], in_=b2.unsqueeze(0))
+                nc.sync.dma_start(out=slope_bf[:], in_=sigmoid_param.partition_broadcast(P))
+            if half == 0 and t == W2_AFTER:
                 for block in range(ROUND_GROUPS // PLANES):
                     load_w2(ROUND_GROUPS // PLANES * part + block)
             if half == 1 and r % 2 == 1:
@@ -214,14 +226,17 @@ def tile_gcnnodeclassifiernetwork_pb_k_kernel(
                 out=rest[:, tile_no, :],
                 in0=g_sum[tile_no][:],
                 scalar=d_sq[:, tile_no : tile_no + 1],
-                in1=rest[:, tile_no, :],
+                in1=b2_all[:] if tile_no < PACK else rest[:, tile_no, :],
                 op0=ALU.mult,
                 op1=ALU.add,
             )
 
         def add_skip(tile_no):
             nc.vector.tensor_tensor(
-                out=rest[:, tile_no, :], in0=rest[:, tile_no, :], in1=x_rows[:, tile_no, :], op=ALU.add
+                out=rest[:, tile_no, :],
+                in0=rest[:, tile_no, :] if tile_no < PACK else b2_all[:],
+                in1=x_rows[:, tile_no, :],
+                op=ALU.add,
             )
 
         def quantise_m(half):
@@ -286,45 +301,49 @@ def tile_gcnnodeclassifiernetwork_pb_k_kernel(
         for r in range(H1_BUFS):
             load_round(r)
 
-        b2_bank = turn_banks.tile([P, CLASSES], F32, name="b2_bank", tag="bank")
-        nc.tensor.matmul(out=b2_bank[:], lhsT=ones[:], rhs=b2_rows[:], start=True, stop=True)
-        b2_all = keep.tile([P, CLASSES], F32, name="b2_all")
-        nc.vector.tensor_copy(out=b2_all[:], in_=b2_bank[:])
-        d = keep.tile([P, TILES], F32, name="d")
-        nc.vector.tensor_copy(out=d[:], in_=d_bf[:].rearrange("p h t -> p (h t)"))
-        d_sq = keep.tile([P, TILES], F32, name="d_sq")
-        nc.vector.tensor_mul(out=d_sq[:], in0=d[:], in1=d[:])
-        slope = keep.tile([P, 1], F32, name="slope")
-        nc.vector.tensor_copy(out=slope[:], in_=slope_bf[:])
+        def prepare_constants():
+            b2_bank = turn_banks.tile([P, CLASSES], F32, name="b2_bank", tag="bank")
+            nc.tensor.matmul(out=b2_bank[:], lhsT=ones[:], rhs=b2_rows[:], start=True, stop=True)
+            nc.vector.tensor_copy(out=b2_all[:], in_=b2_bank[:])
+            nc.vector.tensor_copy(out=d[:], in_=d_bf[:].rearrange("p h t -> p (h t)"))
+            nc.vector.tensor_mul(out=d_sq[:], in0=d[:], in1=d[:])
+            nc.vector.tensor_copy(out=slope[:], in_=slope_bf[:])
 
-        for r in range(AHEAD + 1):
-            sort_round(r)
+        warm_bank = turn_banks.tile([P, CLASSES], F32, name="warm_bank", tag="bank")
+        for i in range(WARM_UP):
+            nc.tensor.matmul(out=warm_bank[:], lhsT=ones[:], rhs=warm_rows[:], start=True, stop=True)
         for r in range(AHEAD):
+            sort_round(r)
             transpose_round(r)
-        for r in range(AHEAD - 1):
-            quantise_round(r)
+        quantise_round(0)
         for r in range(ROUNDS + 2):
-            transpose_round(r + AHEAD)
-            quantise_round(r + AHEAD - 1)
-            sort_round(r + AHEAD + 1)
-            multiply_round(r)
+            if r < LEAD_STEPS:
+                multiply_round(r)
+                sort_round(r + AHEAD)
+                transpose_round(r + AHEAD)
+                quantise_round(r + AHEAD - 1)
+            else:
+                if r == LEAD_STEPS:
+                    sort_round(r + AHEAD)
+                transpose_round(r + AHEAD)
+                quantise_round(r + AHEAD - 1)
+                sort_round(r + AHEAD + 1)
+                multiply_round(r)
+            if r == CONST_STEP:
+                prepare_constants()
             if finished_in(r - 1) is not None:
                 make_message(finished_in(r - 1))
             if finished_in(r - 2) is not None:
                 if finished_in(r - 2) % PACK == PACK - 1:
                     quantise_m(finished_in(r - 2) // PACK)
                 add_self_loop(finished_in(r - 2))
-            if r == B2_STEP:
-                nc.vector.tensor_copy(
-                    out=rest[:], in_=b2_all[:].unsqueeze(1).to_broadcast([P, TILES, CLASSES])
-                )
             if 0 <= r - A_FIRST - 1 < A_QUARTERS:
                 quantise_a(r - A_FIRST - 1)
             if 0 <= r - A_FIRST < A_QUARTERS:
                 regroup_a(r - A_FIRST)
             if X_FIRST <= r < ROUNDS:
-                add_skip(2 * (r - X_FIRST))
-                add_skip(2 * (r - X_FIRST) + 1)
+                add_skip(2 * X_ORDER[r - X_FIRST])
+                add_skip(2 * X_ORDER[r - X_FIRST] + 1)
 
         for tile_no in range(TILES - 1):
             aggregate(tile_no, 0)

@@ -67,7 +67,8 @@ def tile_gcnnodeclassifiernetwork_pb_k_kernel(
         grouped_pool = ctx.enter_context(tc.tile_pool(name="grouped_pool", bufs=2))
         codes_pool = ctx.enter_context(tc.tile_pool(name="codes_pool", bufs=AHEAD + 2))
         a_pool = ctx.enter_context(tc.tile_pool(name="a_pool", bufs=2))
-        out_pool = ctx.enter_context(tc.tile_pool(name="out_pool", bufs=3))
+        h_pool = ctx.enter_context(tc.tile_pool(name="h_pool", bufs=3))
+        out_pool = ctx.enter_context(tc.tile_pool(name="out_pool", bufs=TILES))
         turn_banks = ctx.enter_context(tc.psum_pool(name="turn_banks", bufs=4))
         sum_banks = ctx.enter_context(tc.psum_pool(name="sum_banks", bufs=4))
 
@@ -285,7 +286,7 @@ def tile_gcnnodeclassifiernetwork_pb_k_kernel(
             )
 
         def finish(tile_no):
-            h_plus_x = out_pool.tile([P, CLASSES], F32, name="h_plus_x")
+            h_plus_x = h_pool.tile([P, CLASSES], F32, name="h_plus_x")
             nc.vector.scalar_tensor_tensor(
                 out=h_plus_x[:],
                 in0=agg[tile_no][:],

@@ -31,8 +31,6 @@ PLANES = 4
 W2_BLOCKS = GROUPS // PLANES
 A_QUARTERS = HALVES * HALVES
 W2_AFTER = 2
-SMALL_AFTER = 3
-CONST_STEP = 4
 LEAD_STEPS = 4
 WARM_UP = 8
 AHEAD = 2
@@ -53,7 +51,6 @@ def tile_gcnnodeclassifiernetwork_pb_k_kernel(
     a_view = A.rearrange("(h p t) j -> h p t j", p=P, t=PACK)
     x_view = x.rearrange("(h p t) n -> p h (t n)", p=P, t=PACK)
     out_view = out.rearrange("(h p t) n -> h p t n", p=P, t=PACK)
-    d_view = deg_inv_sqrt.rearrange("(h p t) -> p h t", p=P, t=PACK)
     w2_word_view = (
         W2_words.rearrange("g p n t -> g p (n t)").bitcast(I32).rearrange("g p w -> p g w")
     )
@@ -91,8 +88,13 @@ def tile_gcnnodeclassifiernetwork_pb_k_kernel(
         nc.vector.memset(warm_rows[:], 1.0)
         b2_rows = keep.tile([P, CLASSES], BF16, name="b2_rows")
         nc.vector.memset(b2_rows[:], 0.0)
-        d_bf = keep.tile([P, HALVES, PACK], BF16, name="d_bf")
-        slope_bf = keep.tile([P, 1], BF16, name="slope_bf")
+        d_rows = keep.tile([P, NODES], BF16, name="d_rows")
+        nc.vector.memset(d_rows[:], 0.0)
+        slope_rows = keep.tile([P, 1], BF16, name="slope_rows")
+        nc.vector.memset(slope_rows[:], 0.0)
+        nc.scalar.dma_start(out=b2_rows[0:1, :], in_=b2.unsqueeze(0))
+        nc.scalar.dma_start(out=d_rows[0:1, :], in_=deg_inv_sqrt.unsqueeze(0))
+        nc.scalar.dma_start(out=slope_rows[0:1, :], in_=sigmoid_param.unsqueeze(0))
         b2_all = keep.tile([P, CLASSES], F32, name="b2_all")
         d = keep.tile([P, TILES], F32, name="d")
         d_sq = keep.tile([P, TILES], F32, name="d_sq")
@@ -131,10 +133,6 @@ def tile_gcnnodeclassifiernetwork_pb_k_kernel(
             nc.sync.dma_start(
                 out=h1_raw[r][:], in_=h1_view[half, :, t, ROUND_K * part : ROUND_K * (part + 1)]
             )
-            if r == SMALL_AFTER:
-                nc.sync.dma_start(out=d_bf[:], in_=d_view)
-                nc.sync.dma_start(out=b2_rows[0:1, :], in_=b2.unsqueeze(0))
-                nc.sync.dma_start(out=slope_bf[:], in_=sigmoid_param.partition_broadcast(P))
             if half == 0 and t == W2_AFTER:
                 for block in range(ROUND_GROUPS // PLANES):
                     load_w2(ROUND_GROUPS // PLANES * part + block)
@@ -302,13 +300,30 @@ def tile_gcnnodeclassifiernetwork_pb_k_kernel(
         for r in range(H1_BUFS):
             load_round(r)
 
-        def prepare_constants():
+        def spread_small_inputs():
             b2_bank = turn_banks.tile([P, CLASSES], F32, name="b2_bank", tag="bank")
             nc.tensor.matmul(out=b2_bank[:], lhsT=ones[:], rhs=b2_rows[:], start=True, stop=True)
+            small_bank = turn_banks.tile([P, TILES + 1], F32, name="small_bank", tag="bank")
+            for tile_no in range(TILES):
+                half, t = tile_no // PACK, tile_no % PACK
+                nodes = slice(K_PASS * half + t, K_PASS * (half + 1), PACK)
+                nc.tensor.matmul(
+                    out=small_bank[:, tile_no : tile_no + 1],
+                    lhsT=d_rows[:, nodes],
+                    rhs=ones[:, 0:1],
+                    start=True,
+                    stop=True,
+                )
+            nc.tensor.matmul(
+                out=small_bank[:, TILES : TILES + 1], lhsT=ones[:], rhs=slope_rows[:], start=True, stop=True
+            )
+            return b2_bank, small_bank
+
+        def keep_small_inputs(b2_bank, small_bank):
             nc.vector.tensor_copy(out=b2_all[:], in_=b2_bank[:])
-            nc.vector.tensor_copy(out=d[:], in_=d_bf[:].rearrange("p h t -> p (h t)"))
+            nc.vector.tensor_copy(out=d[:], in_=small_bank[:, 0:TILES])
+            nc.vector.tensor_copy(out=slope[:], in_=small_bank[:, TILES : TILES + 1])
             nc.vector.tensor_mul(out=d_sq[:], in0=d[:], in1=d[:])
-            nc.vector.tensor_copy(out=slope[:], in_=slope_bf[:])
 
         warm_bank = turn_banks.tile([P, CLASSES], F32, name="warm_bank", tag="bank")
         for i in range(WARM_UP):
@@ -316,7 +331,9 @@ def tile_gcnnodeclassifiernetwork_pb_k_kernel(
         for r in range(AHEAD):
             sort_round(r)
             transpose_round(r)
+        small_banks = spread_small_inputs()
         quantise_round(0)
+        keep_small_inputs(*small_banks)
         for r in range(ROUNDS + 2):
             if r < LEAD_STEPS:
                 multiply_round(r)
@@ -330,8 +347,6 @@ def tile_gcnnodeclassifiernetwork_pb_k_kernel(
                 quantise_round(r + AHEAD - 1)
                 sort_round(r + AHEAD + 1)
                 multiply_round(r)
-            if r == CONST_STEP:
-                prepare_constants()
             if finished_in(r - 1) is not None:
                 make_message(finished_in(r - 1))
             if finished_in(r - 2) is not None:

@@ -27,11 +27,15 @@ ROUNDS = HALVES * HALF_ROUNDS
 BANK_GROUPS = 2
 QUADRANT = 32
 QUADRANTS = P // QUADRANT
+MX_ALIGN = 256
 PLANES = 4
 W2_BLOCKS = GROUPS // PLANES
 A_QUARTERS = HALVES * HALVES
 W2_AFTER = 2
-LEAD_STEPS = 4
+LEAD_STEPS = 3
+SMALL_AFTER = 1
+SPREAD = -1
+EARLY = 2
 WARM_UP = 8
 AHEAD = 2
 H1_BUFS = 4
@@ -69,13 +73,13 @@ def tile_gcnnodeclassifiernetwork_pb_k_kernel(
         turn_banks = ctx.enter_context(tc.psum_pool(name="turn_banks", bufs=4))
         sum_banks = ctx.enter_context(tc.psum_pool(name="sum_banks", bufs=4))
 
-        w2_codes = keep.tile([P, GROUPS, CLASSES], U32, name="w2_codes", align_bytes=64)
-        w2_planes = keep.tile([P, W2_BLOCKS, CLASSES], U8, name="w2_planes", align_bytes=64)
-        a_codes = keep.tile([P, HALVES, NODES], U32, name="a_codes", align_bytes=64)
-        a_planes = keep.tile([P, HALVES, NODES], U8, name="a_planes", align_bytes=64)
+        w2_codes = keep.tile([P, GROUPS, CLASSES], U32, name="w2_codes", align_bytes=MX_ALIGN)
+        w2_planes = keep.tile([P, W2_BLOCKS, CLASSES], U8, name="w2_planes", align_bytes=MX_ALIGN)
+        a_codes = keep.tile([P, HALVES, NODES], U32, name="a_codes", align_bytes=MX_ALIGN)
+        a_planes = keep.tile([P, HALVES, NODES], U8, name="a_planes", align_bytes=MX_ALIGN)
         m_grouped = keep.tile([P, HALVES, CLASSES, PACK], BF16, name="m_grouped", align_bytes=64)
-        m_codes = keep.tile([P, HALVES, CLASSES], U32, name="m_codes", align_bytes=64)
-        m_planes = keep.tile([P, HALVES, CLASSES], U8, name="m_planes", align_bytes=64)
+        m_codes = keep.tile([P, HALVES, CLASSES], U32, name="m_codes", align_bytes=MX_ALIGN)
+        m_planes = keep.tile([P, HALVES, CLASSES], U8, name="m_planes", align_bytes=MX_ALIGN)
         x_rows = keep.tile([P, TILES, CLASSES], BF16, name="x_rows")
         rest = keep.tile([P, TILES, CLASSES], F32, name="rest")
 
@@ -86,15 +90,10 @@ def tile_gcnnodeclassifiernetwork_pb_k_kernel(
         nc.vector.memset(ones[:], 1.0)
         warm_rows = keep.tile([P, CLASSES], BF16, name="warm_rows")
         nc.vector.memset(warm_rows[:], 1.0)
-        b2_rows = keep.tile([P, CLASSES], BF16, name="b2_rows")
-        nc.vector.memset(b2_rows[:], 0.0)
-        d_rows = keep.tile([P, NODES], BF16, name="d_rows")
-        nc.vector.memset(d_rows[:], 0.0)
-        slope_rows = keep.tile([P, 1], BF16, name="slope_rows")
-        nc.vector.memset(slope_rows[:], 0.0)
-        nc.scalar.dma_start(out=b2_rows[0:1, :], in_=b2.unsqueeze(0))
-        nc.scalar.dma_start(out=d_rows[0:1, :], in_=deg_inv_sqrt.unsqueeze(0))
-        nc.scalar.dma_start(out=slope_rows[0:1, :], in_=sigmoid_param.unsqueeze(0))
+        small_rows = keep.tile([P, CLASSES], BF16, name="small_rows")
+        nc.vector.memset(small_rows[:], 0.0)
+        ident_bf = keep.tile([P, PACK], BF16, name="ident_bf")
+        nc.vector.tensor_copy(out=ident_bf[:], in_=ident[:, 0:PACK])
         b2_all = keep.tile([P, CLASSES], F32, name="b2_all")
         d = keep.tile([P, TILES], F32, name="d")
         d_sq = keep.tile([P, TILES], F32, name="d_sq")
@@ -133,6 +132,12 @@ def tile_gcnnodeclassifiernetwork_pb_k_kernel(
             nc.sync.dma_start(
                 out=h1_raw[r][:], in_=h1_view[half, :, t, ROUND_K * part : ROUND_K * (part + 1)]
             )
+            if r == SMALL_AFTER:
+                nc.sync.dma_start(out=small_rows[0:1, :], in_=b2.unsqueeze(0))
+                nc.sync.dma_start(
+                    out=small_rows[1 : 1 + HALVES, :], in_=deg_inv_sqrt.rearrange("(h n) -> h n", h=HALVES)
+                )
+                nc.sync.dma_start(out=small_rows[3:4, 0:1], in_=sigmoid_param.unsqueeze(0))
             if half == 0 and t == W2_AFTER:
                 for block in range(ROUND_GROUPS // PLANES):
                     load_w2(ROUND_GROUPS // PLANES * part + block)
@@ -185,8 +190,8 @@ def tile_gcnnodeclassifiernetwork_pb_k_kernel(
         def quantise_round(r):
             if r >= ROUNDS:
                 return
-            h1_codes[r] = codes_pool.tile([P, ROUND_GROUPS * P], U32, name="h1_codes", align_bytes=64)
-            h1_planes[r] = codes_pool.tile([P, ROUND_GROUPS * P], U8, name="h1_planes", align_bytes=64)
+            h1_codes[r] = codes_pool.tile([P, ROUND_GROUPS * P], U32, name="h1_codes", align_bytes=MX_ALIGN)
+            h1_planes[r] = codes_pool.tile([P, ROUND_GROUPS * P], U8, name="h1_planes", align_bytes=MX_ALIGN)
             nc.vector.quantize_mx(
                 out=h1_codes[r][:].bitcast(FP8X4), scales=h1_planes[r][:], in_=grouped[r][:]
             )
@@ -300,28 +305,38 @@ def tile_gcnnodeclassifiernetwork_pb_k_kernel(
         for r in range(H1_BUFS):
             load_round(r)
 
+        small_banks = []
+
         def spread_small_inputs():
             b2_bank = turn_banks.tile([P, CLASSES], F32, name="b2_bank", tag="bank")
-            nc.tensor.matmul(out=b2_bank[:], lhsT=ones[:], rhs=b2_rows[:], start=True, stop=True)
+            nc.tensor.matmul(
+                out=b2_bank[:], lhsT=ident_bf[:, 0:1].to_broadcast([P, P]), rhs=small_rows[:], start=True, stop=True
+            )
             small_bank = turn_banks.tile([P, TILES + 1], F32, name="small_bank", tag="bank")
-            for tile_no in range(TILES):
-                half, t = tile_no // PACK, tile_no % PACK
-                nodes = slice(K_PASS * half + t, K_PASS * (half + 1), PACK)
+            for t in range(PACK):
                 nc.tensor.matmul(
-                    out=small_bank[:, tile_no : tile_no + 1],
-                    lhsT=d_rows[:, nodes],
-                    rhs=ones[:, 0:1],
+                    out=small_bank[:, HALVES * t : HALVES * (t + 1)],
+                    lhsT=small_rows[:, t : K_PASS : PACK],
+                    rhs=ident_bf[:, 1 : 1 + HALVES],
                     start=True,
                     stop=True,
                 )
             nc.tensor.matmul(
-                out=small_bank[:, TILES : TILES + 1], lhsT=ones[:], rhs=slope_rows[:], start=True, stop=True
+                out=small_bank[:, TILES : TILES + 1],
+                lhsT=ident_bf[:, 3:4].to_broadcast([P, P]),
+                rhs=small_rows[:, 0:1],
+                start=True,
+                stop=True,
             )
-            return b2_bank, small_bank
+            small_banks.extend((b2_bank, small_bank))
 
-        def keep_small_inputs(b2_bank, small_bank):
+        def keep_small_inputs():
+            b2_bank, small_bank = small_banks
             nc.vector.tensor_copy(out=b2_all[:], in_=b2_bank[:])
-            nc.vector.tensor_copy(out=d[:], in_=small_bank[:, 0:TILES])
+            nc.vector.tensor_copy(
+                out=d[:].rearrange("p (h t) -> p h t", h=HALVES),
+                in_=small_bank[:, 0:TILES].rearrange("p (t h) -> p h t", h=HALVES),
+            )
             nc.vector.tensor_copy(out=slope[:], in_=small_bank[:, TILES : TILES + 1])
             nc.vector.tensor_mul(out=d_sq[:], in0=d[:], in1=d[:])
 
@@ -331,14 +346,20 @@ def tile_gcnnodeclassifiernetwork_pb_k_kernel(
         for r in range(AHEAD):
             sort_round(r)
             transpose_round(r)
-        small_banks = spread_small_inputs()
+        if SPREAD == -1:
+            spread_small_inputs()
         quantise_round(0)
-        keep_small_inputs(*small_banks)
+        if SPREAD == -1:
+            keep_small_inputs()
+        for r in range(AHEAD, EARLY):
+            sort_round(r)
+            transpose_round(r)
         for r in range(ROUNDS + 2):
             if r < LEAD_STEPS:
                 multiply_round(r)
-                sort_round(r + AHEAD)
-                transpose_round(r + AHEAD)
+                if r + AHEAD >= EARLY:
+                    sort_round(r + AHEAD)
+                    transpose_round(r + AHEAD)
                 quantise_round(r + AHEAD - 1)
             else:
                 if r == LEAD_STEPS:
@@ -347,6 +368,9 @@ def tile_gcnnodeclassifiernetwork_pb_k_kernel(
                 quantise_round(r + AHEAD - 1)
                 sort_round(r + AHEAD + 1)
                 multiply_round(r)
+            if r == SPREAD:
+                spread_small_inputs()
+                keep_small_inputs()
             if finished_in(r - 1) is not None:
                 make_message(finished_in(r - 1))
             if finished_in(r - 2) is not None:

@@ -30,6 +30,13 @@ QUADRANTS = P // QUADRANT
 MX_ALIGN = 256
 PLANES = 4
 W2_BLOCKS = GROUPS // PLANES
+LAST = TILES - 1
+SECOND_HALF = [(1, part, t) for part in range(PARTS) for t in range(PACK - 1)] + [
+    (1, part, PACK - 1) for part in range(PARTS)
+]
+LAST_ROUNDS = range(ROUNDS - PARTS, ROUNDS)
+HALF_CLASSES = CLASSES // 2
+ALL, LOW, HIGH = slice(0, CLASSES), slice(0, HALF_CLASSES), slice(HALF_CLASSES, CLASSES)
 A_QUARTERS = HALVES * HALVES
 W2_AFTER = 2
 LEAD_STEPS = 3
@@ -41,7 +48,7 @@ AHEAD = 2
 H1_BUFS = 4
 A_FIRST = HALF_ROUNDS
 X_FIRST = ROUNDS - TILES // 2
-X_ORDER = (2, 3, 0, 1)
+X_ORDER = (2, 3, 0)
 
 FLOPS = 2 * NODES * HIDDEN * CLASSES + 2 * NODES * NODES * CLASSES
 
@@ -103,7 +110,9 @@ def tile_gcnnodeclassifiernetwork_pb_k_kernel(
         nc.scalar.activation(out=warm[:], in_=warm[:], func=ACT.Sigmoid)
 
         def where(r):
-            return r // HALF_ROUNDS, (r // PACK) % PARTS, r % PACK
+            if r < HALF_ROUNDS:
+                return 0, r // PACK, r % PACK
+            return SECOND_HALF[r - HALF_ROUNDS]
 
         def finished_in(r):
             if r < 0 or r >= ROUNDS:
@@ -198,39 +207,47 @@ def tile_gcnnodeclassifiernetwork_pb_k_kernel(
 
         g_sum = {}
 
-        def multiply_round(r):
+        def columns_in_loop(tile_no):
+            return ALL if tile_no < LAST else LOW
+
+        def multiply_round(r, cols=None):
             if r >= ROUNDS:
                 return
             half, part, t = where(r)
             tile_no = PACK * half + t
+            cols = cols or columns_in_loop(tile_no)
             if part == 0:
-                g_sum[tile_no] = sum_banks.tile([P, CLASSES], F32, name="g_sum", tag="sums")
+                if cols == HIGH:
+                    bank = turn_banks.tile([P, CLASSES], F32, name="g_high", tag="bank")
+                else:
+                    bank = sum_banks.tile([P, CLASSES], F32, name="g_sum", tag="sums")
+                g_sum[tile_no, cols.start] = bank[:, 0 : cols.stop - cols.start]
             for g in range(ROUND_GROUPS):
                 group = ROUND_GROUPS * part + g
                 nc.tensor.matmul_mx(
-                    out=g_sum[tile_no][:],
+                    out=g_sum[tile_no, cols.start],
                     lhsT=h1_codes[r][:, P * g : P * (g + 1)].bitcast(FP8X4),
                     lhsT_scale=h1_planes[r][:, P * g : P * (g + 1)],
-                    rhs=w2_codes[:, group, :].bitcast(FP8X4),
-                    rhs_scale=w2_planes[PACK * (group % PLANES) : P, group // PLANES, :],
+                    rhs=w2_codes[:, group, cols].bitcast(FP8X4),
+                    rhs_scale=w2_planes[PACK * (group % PLANES) : P, group // PLANES, cols],
                     start=(group == 0),
                     stop=(group == GROUPS - 1),
                 )
 
-        def make_message(tile_no):
+        def make_message(tile_no, cols):
             nc.scalar.activation(
-                out=m_grouped[:, tile_no // PACK, :, tile_no % PACK],
-                in_=g_sum[tile_no][:],
+                out=m_grouped[:, tile_no // PACK, cols, tile_no % PACK],
+                in_=g_sum[tile_no, cols.start],
                 func=ACT.Copy,
                 scale=d[:, tile_no : tile_no + 1],
             )
 
-        def add_self_loop(tile_no):
+        def add_self_loop(tile_no, cols):
             nc.vector.scalar_tensor_tensor(
-                out=rest[:, tile_no, :],
-                in0=g_sum[tile_no][:],
+                out=rest[:, tile_no, cols],
+                in0=g_sum[tile_no, cols.start],
                 scalar=d_sq[:, tile_no : tile_no + 1],
-                in1=b2_all[:] if tile_no < PACK else rest[:, tile_no, :],
+                in1=b2_all[:, cols] if tile_no < PACK else rest[:, tile_no, cols],
                 op0=ALU.mult,
                 op1=ALU.add,
             )
@@ -243,11 +260,11 @@ def tile_gcnnodeclassifiernetwork_pb_k_kernel(
                 op=ALU.add,
             )
 
-        def quantise_m(half):
+        def quantise_m(half, cols):
             nc.vector.quantize_mx(
-                out=m_codes[:, half, :].bitcast(FP8X4),
-                scales=m_planes[:, half, :],
-                in_=m_grouped[:, half, :, :].rearrange("p n t -> p (n t)"),
+                out=m_codes[:, half, cols].bitcast(FP8X4),
+                scales=m_planes[:, half, cols],
+                in_=m_grouped[:, half, cols, :].rearrange("p n t -> p (n t)"),
             )
 
         a_grouped = {}
@@ -273,34 +290,37 @@ def tile_gcnnodeclassifiernetwork_pb_k_kernel(
 
         agg = {}
 
-        def aggregate(tile_no, half):
-            if half == 0:
-                banks, tag = (turn_banks, "bank") if tile_no < PACK else (sum_banks, "sums")
-                agg[tile_no] = banks.tile([P, CLASSES], F32, name="agg", tag=tag)
-            cols = slice(P * tile_no, P * (tile_no + 1))
-            nc.tensor.matmul_mx(
-                out=agg[tile_no][:],
-                lhsT=a_codes[:, half, cols].bitcast(FP8X4),
-                lhsT_scale=a_planes[:, half, cols],
-                rhs=m_codes[:, half, :].bitcast(FP8X4),
-                rhs_scale=m_planes[:, half, :],
-                start=(half == 0),
-                stop=(half == HALVES - 1),
-            )
+        def aggregate(pair, cols):
+            banks, tag = (sum_banks, "sums") if pair < PACK else (turn_banks, "bank")
+            agg[pair, cols.start] = banks.tile([P, 2, HALF_CLASSES], F32, name="agg", tag=tag)
+            for i in range(2):
+                targets = slice(P * (pair + i), P * (pair + i + 1))
+                for half in range(HALVES):
+                    nc.tensor.matmul_mx(
+                        out=agg[pair, cols.start][:, i, :],
+                        lhsT=a_codes[:, half, targets].bitcast(FP8X4),
+                        lhsT_scale=a_planes[:, half, targets],
+                        rhs=m_codes[:, half, cols].bitcast(FP8X4),
+                        rhs_scale=m_planes[:, half, cols],
+                        start=(half == 0),
+                        stop=(half == HALVES - 1),
+                    )
 
-        def finish(tile_no):
-            h_plus_x = h_pool.tile([P, CLASSES], F32, name="h_plus_x")
-            nc.vector.scalar_tensor_tensor(
-                out=h_plus_x[:],
-                in0=agg[tile_no][:],
-                scalar=d[:, tile_no : tile_no + 1],
-                in1=rest[:, tile_no, :],
-                op0=ALU.mult,
-                op1=ALU.add,
-            )
-            result = out_pool.tile([P, CLASSES], F32, name="result")
+        def finish(pair, cols):
+            h_plus_x = h_pool.tile([P, 2, HALF_CLASSES], F32, name="h_plus_x")
+            for i in range(2):
+                nc.vector.scalar_tensor_tensor(
+                    out=h_plus_x[:, i, :],
+                    in0=agg[pair, cols.start][:, i, :],
+                    scalar=d[:, pair + i : pair + i + 1],
+                    in1=rest[:, pair + i, cols],
+                    op0=ALU.mult,
+                    op1=ALU.add,
+                )
+            result = out_pool.tile([P, 2, HALF_CLASSES], F32, name="result")
             nc.scalar.activation(out=result[:], in_=h_plus_x[:], func=ACT.Sigmoid, scale=slope[:, 0:1])
-            nc.sync.dma_start(out=out_view[tile_no // PACK, :, tile_no % PACK, :], in_=result[:])
+            t = pair % PACK
+            nc.sync.dma_start(out=out_view[pair // PACK, :, t : t + 2, cols], in_=result[:])
 
         for r in range(H1_BUFS):
             load_round(r)
@@ -354,7 +374,7 @@ def tile_gcnnodeclassifiernetwork_pb_k_kernel(
         for r in range(AHEAD, EARLY):
             sort_round(r)
             transpose_round(r)
-        for r in range(ROUNDS + 2):
+        for r in range(ROUNDS):
             if r < LEAD_STEPS:
                 multiply_round(r)
                 if r + AHEAD >= EARLY:
@@ -372,24 +392,35 @@ def tile_gcnnodeclassifiernetwork_pb_k_kernel(
                 spread_small_inputs()
                 keep_small_inputs()
             if finished_in(r - 1) is not None:
-                make_message(finished_in(r - 1))
+                make_message(finished_in(r - 1), ALL)
             if finished_in(r - 2) is not None:
-                if finished_in(r - 2) % PACK == PACK - 1:
-                    quantise_m(finished_in(r - 2) // PACK)
-                add_self_loop(finished_in(r - 2))
+                if finished_in(r - 2) == PACK - 1:
+                    quantise_m(0, ALL)
+                add_self_loop(finished_in(r - 2), ALL)
             if 0 <= r - A_FIRST - 1 < A_QUARTERS:
                 quantise_a(r - A_FIRST - 1)
             if 0 <= r - A_FIRST < A_QUARTERS:
                 regroup_a(r - A_FIRST)
-            if X_FIRST <= r < ROUNDS:
+            if 0 <= r - X_FIRST < len(X_ORDER):
                 add_skip(2 * X_ORDER[r - X_FIRST])
                 add_skip(2 * X_ORDER[r - X_FIRST] + 1)
 
-        for tile_no in range(TILES - 1):
-            aggregate(tile_no, 0)
-        for tile_no in range(TILES - 1):
-            aggregate(tile_no, 1)
-            finish(tile_no)
-        aggregate(TILES - 1, 0)
-        aggregate(TILES - 1, 1)
-        finish(TILES - 1)
+        for r in LAST_ROUNDS:
+            multiply_round(r, HIGH)
+        make_message(LAST, LOW)
+        quantise_m(1, LOW)
+        add_self_loop(LAST, LOW)
+        add_skip(2)
+        add_skip(3)
+        for pair in range(0, TILES, 2):
+            aggregate(pair, LOW)
+        make_message(LAST, HIGH)
+        finish(0, LOW)
+        quantise_m(1, HIGH)
+        add_self_loop(LAST, HIGH)
+        for pair in range(0, TILES, 2):
+            aggregate(pair, HIGH)
+        for pair in range(2, TILES, 2):
+            finish(pair, LOW)
+        for pair in range(0, TILES, 2):
+            finish(pair, HIGH)

@@ -40,6 +40,7 @@ ALL, LOW, HIGH = slice(0, CLASSES), slice(0, HALF_CLASSES), slice(HALF_CLASSES, 
 A_QUARTERS = HALVES * HALVES
 W2_AFTER = 2
 LEAD_STEPS = 3
+STEP2 = (12, 14)
 SMALL_AFTER = 1
 SPREAD = -1
 EARLY = 2
@@ -162,8 +163,11 @@ def tile_gcnnodeclassifiernetwork_pb_k_kernel(
 
         sorted_words = {}
 
+        def words_of(r):
+            return h1_raw[r][:].bitcast(F32).rearrange("p (g q u) -> p g u q", g=ROUND_GROUPS, u=2)
+
         def sort_round(r):
-            if r >= ROUNDS:
+            if r >= ROUNDS or r in STEP2:
                 return
             sorted_words[r] = sorted_pool.tile([P, ROUND_GROUPS, 2, P], F32, name="sorted_words")
             nc.vector.tensor_copy(
@@ -186,12 +190,17 @@ def tile_gcnnodeclassifiernetwork_pb_k_kernel(
                 for i in range(BANK_GROUPS):
                     for u in range(2):
                         nc.tensor.transpose(
-                            bank[:, i, u, :], sorted_words[r][:, first + i, u, :], ident[:]
+                            bank[:, i, u, :],
+                            (words_of(r) if r in STEP2 else sorted_words[r])[:, first + i, u, :],
+                            ident[:],
                         )
                 nc.scalar.copy(
                     out=grouped_words[:, first : first + BANK_GROUPS, :, :],
                     in_=bank[:].rearrange("p i u n -> p i n u"),
                 )
+
+            if r in STEP2:
+                load_round(r + H1_BUFS)
 
         h1_codes = {}
         h1_planes = {}

from contextlib import ExitStack

import concourse.mybir as mybir
from concourse.masks import make_identity

F32 = mybir.dt.float32
BF16 = mybir.dt.bfloat16
U8 = mybir.dt.uint8
U32 = mybir.dt.uint32
I32 = mybir.dt.int32
FP8X4 = mybir.dt.float8_e4m3fn_x4
ACT = mybir.ActivationFunctionType
ALU = mybir.AluOpType

P = 128
PACK = 4
K_PASS = P * PACK
NODES, HIDDEN, CLASSES = 1024, 8192, 512
HALVES = NODES // K_PASS
TILES = HALVES * PACK
GROUPS = HIDDEN // K_PASS
ROUND_GROUPS = 8
ROUND_K = ROUND_GROUPS * K_PASS
PARTS = GROUPS // ROUND_GROUPS
HALF_ROUNDS = PARTS * PACK
ROUNDS = HALVES * HALF_ROUNDS
BANK_GROUPS = 2
QUADRANT = 32
QUADRANTS = P // QUADRANT
MX_ALIGN = 256
PLANES = 4
W2_BLOCKS = GROUPS // PLANES
LAST = TILES - 1
SECOND_HALF = [(1, part, t) for part in range(PARTS) for t in range(PACK - 1)] + [
    (1, part, PACK - 1) for part in range(PARTS)
]
LAST_ROUNDS = range(ROUNDS - PARTS, ROUNDS)
HALF_CLASSES = CLASSES // 2
ALL, LOW, HIGH = slice(0, CLASSES), slice(0, HALF_CLASSES), slice(HALF_CLASSES, CLASSES)
A_QUARTERS = HALVES * HALVES
W2_AFTER = 2
LEAD_STEPS = 3
STEP2 = (12, 14)
SMALL_AFTER = 1
SPREAD = -1
EARLY = 2
WARM_UP = 8
AHEAD = 2
H1_BUFS = 4
A_FIRST = HALF_ROUNDS
X_FIRST = ROUNDS - TILES // 2
X_ORDER = (2, 3, 0)

FLOPS = 2 * NODES * HIDDEN * CLASSES + 2 * NODES * NODES * CLASSES


def tile_gcnnodeclassifiernetwork_pb_k_kernel(
    tc, A, deg_inv_sqrt, h1, W2_words, W2_scales, b2, x, sigmoid_param, out
):
    nc = tc.nc

    h1_view = h1.rearrange("(h p t) k -> h p t k", p=P, t=PACK)
    a_view = A.rearrange("(h p t) j -> h p t j", p=P, t=PACK)
    x_view = x.rearrange("(h p t) n -> p h (t n)", p=P, t=PACK)
    out_view = out.rearrange("(h p t) n -> h p t n", p=P, t=PACK)
    w2_word_view = (
        W2_words.rearrange("g p n t -> g p (n t)").bitcast(I32).rearrange("g p w -> p g w")
    )
    w2_scale_view = W2_scales.bitcast(I32)

    with ExitStack() as ctx:
        ctx.enter_context(tc.manual_schedule())
        keep = ctx.enter_context(tc.tile_pool(name="keep", bufs=1))
        h1_pool = ctx.enter_context(tc.tile_pool(name="h1_pool", bufs=H1_BUFS))
        sorted_pool = ctx.enter_context(tc.tile_pool(name="sorted_pool", bufs=2))
        grouped_pool = ctx.enter_context(tc.tile_pool(name="grouped_pool", bufs=2))
        codes_pool = ctx.enter_context(tc.tile_pool(name="codes_pool", bufs=AHEAD + 2))
        a_pool = ctx.enter_context(tc.tile_pool(name="a_pool", bufs=2))
        h_pool = ctx.enter_context(tc.tile_pool(name="h_pool", bufs=3))
        out_pool = ctx.enter_context(tc.tile_pool(name="out_pool", bufs=TILES))
        turn_banks = ctx.enter_context(tc.psum_pool(name="turn_banks", bufs=4))
        sum_banks = ctx.enter_context(tc.psum_pool(name="sum_banks", bufs=4))

        w2_codes = keep.tile([P, GROUPS, CLASSES], U32, name="w2_codes", align_bytes=MX_ALIGN)
        w2_planes = keep.tile([P, W2_BLOCKS, CLASSES], U8, name="w2_planes", align_bytes=MX_ALIGN)
        a_codes = keep.tile([P, HALVES, NODES], U32, name="a_codes", align_bytes=MX_ALIGN)
        a_planes = keep.tile([P, HALVES, NODES], U8, name="a_planes", align_bytes=MX_ALIGN)
        m_grouped = keep.tile([P, HALVES, CLASSES, PACK], BF16, name="m_grouped", align_bytes=64)
        m_codes = keep.tile([P, HALVES, CLASSES], U32, name="m_codes", align_bytes=MX_ALIGN)
        m_planes = keep.tile([P, HALVES, CLASSES], U8, name="m_planes", align_bytes=MX_ALIGN)
        x_rows = keep.tile([P, TILES, CLASSES], BF16, name="x_rows")
        rest = keep.tile([P, TILES, CLASSES], F32, name="rest")

        nc.vector.memset(w2_planes[:].bitcast(I32), 0)
        ident = keep.tile([P, P], F32, name="ident")
        make_identity(nc, ident[:])
        ones = keep.tile([P, P], BF16, name="ones")
        nc.vector.memset(ones[:], 1.0)
        warm_rows = keep.tile([P, CLASSES], BF16, name="warm_rows")
        nc.vector.memset(warm_rows[:], 1.0)
        small_rows = keep.tile([P, CLASSES], BF16, name="small_rows")
        nc.vector.memset(small_rows[:], 0.0)
        ident_bf = keep.tile([P, PACK], BF16, name="ident_bf")
        nc.vector.tensor_copy(out=ident_bf[:], in_=ident[:, 0:PACK])
        b2_all = keep.tile([P, CLASSES], F32, name="b2_all")
        d = keep.tile([P, TILES], F32, name="d")
        d_sq = keep.tile([P, TILES], F32, name="d_sq")
        slope = keep.tile([P, 1], F32, name="slope")
        warm = keep.tile([P, 1], F32, name="warm")
        nc.vector.memset(warm[:], 0.0)
        nc.scalar.activation(out=warm[:], in_=warm[:], func=ACT.Sigmoid)

        def where(r):
            if r < HALF_ROUNDS:
                return 0, r // PACK, r % PACK
            return SECOND_HALF[r - HALF_ROUNDS]

        def finished_in(r):
            if r < 0 or r >= ROUNDS:
                return None
            half, part, t = where(r)
            return PACK * half + t if part == PARTS - 1 else None

        def load_w2(block):
            groups = slice(PLANES * block, PLANES * (block + 1))
            for quadrant in range(QUADRANTS):
                rows = slice(QUADRANT * quadrant, QUADRANT * quadrant + PLANES * PACK)
                nc.sync.dma_start(
                    out=w2_planes[rows, block, :].bitcast(I32),
                    in_=w2_scale_view[groups, PACK * quadrant : PACK * (quadrant + 1), :],
                )
            nc.sync.dma_start(out=w2_codes[:, groups, :].bitcast(I32), in_=w2_word_view[:, groups, :])

        a_raw = {}
        h1_raw = {}

        def load_round(r):
            if r >= ROUNDS:
                return
            half, part, t = where(r)
            h1_raw[r] = h1_pool.tile([P, ROUND_K], BF16, name="h1_raw")
            nc.sync.dma_start(
                out=h1_raw[r][:], in_=h1_view[half, :, t, ROUND_K * part : ROUND_K * (part + 1)]
            )
            if r == SMALL_AFTER:
                nc.sync.dma_start(out=small_rows[0:1, :], in_=b2.unsqueeze(0))
                nc.sync.dma_start(
                    out=small_rows[1 : 1 + HALVES, :], in_=deg_inv_sqrt.rearrange("(h n) -> h n", h=HALVES)
                )
                nc.sync.dma_start(out=small_rows[3:4, 0:1], in_=sigmoid_param.unsqueeze(0))
            if half == 0 and t == W2_AFTER:
                for block in range(ROUND_GROUPS // PLANES):
                    load_w2(ROUND_GROUPS // PLANES * part + block)
            if half == 1 and r % 2 == 1:
                late = (r - HALF_ROUNDS) // 2
                if late < HALVES:
                    a_raw[late] = a_pool.tile([P, PACK, NODES], BF16, name="a_raw")
                    nc.sync.dma_start(out=a_raw[late][:], in_=a_view[late])
                if late == HALVES:
                    nc.sync.dma_start(
                        out=x_rows[:].rearrange("p (h t) n -> p h (t n)", h=HALVES), in_=x_view
                    )

        sorted_words = {}

        def words_of(r):
            return h1_raw[r][:].bitcast(F32).rearrange("p (g q u) -> p g u q", g=ROUND_GROUPS, u=2)

        def sort_round(r):
            if r >= ROUNDS or r in STEP2:
                return
            sorted_words[r] = sorted_pool.tile([P, ROUND_GROUPS, 2, P], F32, name="sorted_words")
            nc.vector.tensor_copy(
                out=sorted_words[r][:],
                in_=h1_raw[r][:].bitcast(F32).rearrange("p (g q u) -> p g u q", g=ROUND_GROUPS, u=2),
            )
            load_round(r + H1_BUFS)

        grouped = {}

        def transpose_round(r):
            if r >= ROUNDS:
                return
            grouped[r] = grouped_pool.tile([P, ROUND_K], BF16, name="grouped", align_bytes=64)
            grouped_words = grouped[r][:].bitcast(F32).rearrange(
                "p (g n u) -> p g n u", g=ROUND_GROUPS, u=2
            )
            for first in range(0, ROUND_GROUPS, BANK_GROUPS):
                bank = turn_banks.tile([P, BANK_GROUPS, 2, P], F32, name="bank", tag="bank")
                for i in range(BANK_GROUPS):
                    for u in range(2):
                        nc.tensor.transpose(
                            bank[:, i, u, :],
                            (words_of(r) if r in STEP2 else sorted_words[r])[:, first + i, u, :],
                            ident[:],
                        )
                nc.scalar.copy(
                    out=grouped_words[:, first : first + BANK_GROUPS, :, :],
                    in_=bank[:].rearrange("p i u n -> p i n u"),
                )

            if r in STEP2:
                load_round(r + H1_BUFS)

        h1_codes = {}
        h1_planes = {}

        def quantise_round(r):
            if r >= ROUNDS:
                return
            h1_codes[r] = codes_pool.tile([P, ROUND_GROUPS * P], U32, name="h1_codes", align_bytes=MX_ALIGN)
            h1_planes[r] = codes_pool.tile([P, ROUND_GROUPS * P], U8, name="h1_planes", align_bytes=MX_ALIGN)
            nc.vector.quantize_mx(
                out=h1_codes[r][:].bitcast(FP8X4), scales=h1_planes[r][:], in_=grouped[r][:]
            )

        g_sum = {}

        def columns_in_loop(tile_no):
            return ALL if tile_no < LAST else LOW

        def multiply_round(r, cols=None):
            if r >= ROUNDS:
                return
            half, part, t = where(r)
            tile_no = PACK * half + t
            cols = cols or columns_in_loop(tile_no)
            if part == 0:
                if cols == HIGH:
                    bank = turn_banks.tile([P, CLASSES], F32, name="g_high", tag="bank")
                else:
                    bank = sum_banks.tile([P, CLASSES], F32, name="g_sum", tag="sums")
                g_sum[tile_no, cols.start] = bank[:, 0 : cols.stop - cols.start]
            for g in range(ROUND_GROUPS):
                group = ROUND_GROUPS * part + g
                nc.tensor.matmul_mx(
                    out=g_sum[tile_no, cols.start],
                    lhsT=h1_codes[r][:, P * g : P * (g + 1)].bitcast(FP8X4),
                    lhsT_scale=h1_planes[r][:, P * g : P * (g + 1)],
                    rhs=w2_codes[:, group, cols].bitcast(FP8X4),
                    rhs_scale=w2_planes[PACK * (group % PLANES) : P, group // PLANES, cols],
                    start=(group == 0),
                    stop=(group == GROUPS - 1),
                )

        def make_message(tile_no, cols):
            nc.scalar.activation(
                out=m_grouped[:, tile_no // PACK, cols, tile_no % PACK],
                in_=g_sum[tile_no, cols.start],
                func=ACT.Copy,
                scale=d[:, tile_no : tile_no + 1],
            )

        def add_self_loop(tile_no, cols):
            nc.vector.scalar_tensor_tensor(
                out=rest[:, tile_no, cols],
                in0=g_sum[tile_no, cols.start],
                scalar=d_sq[:, tile_no : tile_no + 1],
                in1=b2_all[:, cols] if tile_no < PACK else rest[:, tile_no, cols],
                op0=ALU.mult,
                op1=ALU.add,
            )

        def add_skip(tile_no):
            nc.vector.tensor_tensor(
                out=rest[:, tile_no, :],
                in0=rest[:, tile_no, :] if tile_no < PACK else b2_all[:],
                in1=x_rows[:, tile_no, :],
                op=ALU.add,
            )

        def quantise_m(half, cols):
            nc.vector.quantize_mx(
                out=m_codes[:, half, cols].bitcast(FP8X4),
                scales=m_planes[:, half, cols],
                in_=m_grouped[:, half, cols, :].rearrange("p n t -> p (n t)"),
            )

        a_grouped = {}

        def regroup_a(quarter):
            half, c = quarter // HALVES, quarter % HALVES
            a_grouped[quarter] = a_pool.tile([P, K_PASS * PACK], BF16, name="a_grouped", align_bytes=64)
            dst = a_grouped[quarter][:].rearrange("p (t2 p2 t) -> p t2 p2 t", t2=PACK, t=PACK)
            src = a_raw[half][:, :, K_PASS * c : K_PASS * (c + 1)].rearrange(
                "p t (p2 t2) -> p t2 p2 t", t2=PACK
            )
            nc.scalar.copy(out=dst[:, 0 : PACK // 2, :, :], in_=src[:, 0 : PACK // 2, :, :])
            nc.vector.tensor_copy(out=dst[:, PACK // 2 : PACK, :, :], in_=src[:, PACK // 2 : PACK, :, :])

        def quantise_a(quarter):
            half, c = quarter // HALVES, quarter % HALVES
            cols = slice(K_PASS * c, K_PASS * (c + 1))
            nc.vector.quantize_mx(
                out=a_codes[:, half, cols].bitcast(FP8X4),
                scales=a_planes[:, half, cols],
                in_=a_grouped[quarter][:],
            )

        agg = {}

        def aggregate(pair, cols):
            banks, tag = (sum_banks, "sums") if pair < PACK else (turn_banks, "bank")
            agg[pair, cols.start] = banks.tile([P, 2, HALF_CLASSES], F32, name="agg", tag=tag)
            for i in range(2):
                targets = slice(P * (pair + i), P * (pair + i + 1))
                for half in range(HALVES):
                    nc.tensor.matmul_mx(
                        out=agg[pair, cols.start][:, i, :],
                        lhsT=a_codes[:, half, targets].bitcast(FP8X4),
                        lhsT_scale=a_planes[:, half, targets],
                        rhs=m_codes[:, half, cols].bitcast(FP8X4),
                        rhs_scale=m_planes[:, half, cols],
                        start=(half == 0),
                        stop=(half == HALVES - 1),
                    )

        def finish(pair, cols):
            h_plus_x = h_pool.tile([P, 2, HALF_CLASSES], F32, name="h_plus_x")
            for i in range(2):
                nc.vector.scalar_tensor_tensor(
                    out=h_plus_x[:, i, :],
                    in0=agg[pair, cols.start][:, i, :],
                    scalar=d[:, pair + i : pair + i + 1],
                    in1=rest[:, pair + i, cols],
                    op0=ALU.mult,
                    op1=ALU.add,
                )
            result = out_pool.tile([P, 2, HALF_CLASSES], F32, name="result")
            nc.scalar.activation(out=result[:], in_=h_plus_x[:], func=ACT.Sigmoid, scale=slope[:, 0:1])
            t = pair % PACK
            nc.sync.dma_start(out=out_view[pair // PACK, :, t : t + 2, cols], in_=result[:])

        for r in range(H1_BUFS):
            load_round(r)

        small_banks = []

        def spread_small_inputs():
            b2_bank = turn_banks.tile([P, CLASSES], F32, name="b2_bank", tag="bank")
            nc.tensor.matmul(
                out=b2_bank[:], lhsT=ident_bf[:, 0:1].to_broadcast([P, P]), rhs=small_rows[:], start=True, stop=True
            )
            small_bank = turn_banks.tile([P, TILES + 1], F32, name="small_bank", tag="bank")
            for t in range(PACK):
                nc.tensor.matmul(
                    out=small_bank[:, HALVES * t : HALVES * (t + 1)],
                    lhsT=small_rows[:, t : K_PASS : PACK],
                    rhs=ident_bf[:, 1 : 1 + HALVES],
                    start=True,
                    stop=True,
                )
            nc.tensor.matmul(
                out=small_bank[:, TILES : TILES + 1],
                lhsT=ident_bf[:, 3:4].to_broadcast([P, P]),
                rhs=small_rows[:, 0:1],
                start=True,
                stop=True,
            )
            small_banks.extend((b2_bank, small_bank))

        def keep_small_inputs():
            b2_bank, small_bank = small_banks
            nc.vector.tensor_copy(out=b2_all[:], in_=b2_bank[:])
            nc.vector.tensor_copy(
                out=d[:].rearrange("p (h t) -> p h t", h=HALVES),
                in_=small_bank[:, 0:TILES].rearrange("p (t h) -> p h t", h=HALVES),
            )
            nc.vector.tensor_copy(out=slope[:], in_=small_bank[:, TILES : TILES + 1])
            nc.vector.tensor_mul(out=d_sq[:], in0=d[:], in1=d[:])

        warm_bank = turn_banks.tile([P, CLASSES], F32, name="warm_bank", tag="bank")
        for i in range(WARM_UP):
            nc.tensor.matmul(out=warm_bank[:], lhsT=ones[:], rhs=warm_rows[:], start=True, stop=True)
        for r in range(AHEAD):
            sort_round(r)
            transpose_round(r)
        if SPREAD == -1:
            spread_small_inputs()
        quantise_round(0)
        if SPREAD == -1:
            keep_small_inputs()
        for r in range(AHEAD, EARLY):
            sort_round(r)
            transpose_round(r)
        for r in range(ROUNDS):
            if r < LEAD_STEPS:
                multiply_round(r)
                if r + AHEAD >= EARLY:
                    sort_round(r + AHEAD)
                    transpose_round(r + AHEAD)
                quantise_round(r + AHEAD - 1)
            else:
                if r == LEAD_STEPS:
                    sort_round(r + AHEAD)
                transpose_round(r + AHEAD)
                quantise_round(r + AHEAD - 1)
                sort_round(r + AHEAD + 1)
                multiply_round(r)
            if r == SPREAD:
                spread_small_inputs()
                keep_small_inputs()
            if finished_in(r - 1) is not None:
                make_message(finished_in(r - 1), ALL)
            if finished_in(r - 2) is not None:
                if finished_in(r - 2) == PACK - 1:
                    quantise_m(0, ALL)
                add_self_loop(finished_in(r - 2), ALL)
            if 0 <= r - A_FIRST - 1 < A_QUARTERS:
                quantise_a(r - A_FIRST - 1)
            if 0 <= r - A_FIRST < A_QUARTERS:
                regroup_a(r - A_FIRST)
            if 0 <= r - X_FIRST < len(X_ORDER):
                add_skip(2 * X_ORDER[r - X_FIRST])
                add_skip(2 * X_ORDER[r - X_FIRST] + 1)

        for r in LAST_ROUNDS:
            multiply_round(r, HIGH)
        make_message(LAST, LOW)
        quantise_m(1, LOW)
        add_self_loop(LAST, LOW)
        add_skip(2)
        add_skip(3)
        for pair in range(0, TILES, 2):
            aggregate(pair, LOW)
        make_message(LAST, HIGH)
        finish(0, LOW)
        quantise_m(1, HIGH)
        add_self_loop(LAST, HIGH)
        for pair in range(0, TILES, 2):
            aggregate(pair, HIGH)
        for pair in range(2, TILES, 2):
            finish(pair, LOW)
        for pair in range(0, TILES, 2):
            finish(pair, HIGH)
